import numpy as np
import ml_dtypes


def mxq(x, axis, fmt="e4m3"):
    dtype, down = {"e4m3": (ml_dtypes.float8_e4m3fn, 7), "e5m2": (ml_dtypes.float8_e5m2, 14)}[fmt]
    v = np.moveaxis(np.asarray(x, np.float32).astype(ml_dtypes.bfloat16).astype(np.float64), axis, -1)
    blocks = v.reshape(v.shape[:-1] + (-1, 32))
    amax = np.abs(blocks).max(-1, keepdims=True)
    byte = np.maximum(np.where(amax > 0, np.frexp(amax)[1] - 1 + 127, 0) - down, 1)
    scale = np.exp2(byte - 127.0)
    codes = (blocks / scale).astype(np.float32).astype(dtype).astype(np.float64)
    return np.moveaxis((codes * scale).reshape(v.shape), -1, axis)


WIDE = False


def mx_kscale(k):
    if not WIDE:
        return np.ones(k)
    levels = np.array([10, -10, 5, -5, 0])
    if k % 512:
        return np.exp2(np.random.permutation(np.resize(levels, k // 32))).repeat(32)
    a = np.empty((k // 512, 16))
    for p in range(k // 512):
        a[p, :8] = np.random.permutation(np.resize(levels, 8))
        for g in range(8):
            far = levels[np.abs(levels - a[p, g]) >= 10]
            a[p, g + 8] = far[np.random.randint(len(far))]
    return np.exp2(a.ravel()).repeat(32)


BF16 = ml_dtypes.bfloat16


def bf(x):
    return np.asarray(x, np.float32).astype(BF16)


def f64(x):
    return np.asarray(x).astype(np.float64)


BATCH, ROWS, COLS, IN_DIM, OUT_DIM = 2, 64, 64, 512, 512
N = ROWS * COLS
EPS_BN = 1e-5
EPS_DEG = 1e-5


def _stencil9(x):
    R, C = x.shape[-3], x.shape[-2]
    pad = [(0, 0)] * (x.ndim - 3) + [(1, 1), (1, 1), (0, 0)]
    xp = np.pad(x, pad)
    out = np.zeros_like(x)
    for di in range(3):
        for dj in range(3):
            out = out + xp[..., di:di + R, dj:dj + C, :]
    return out


def _deg_inv_sqrt(rows, cols):
    D = _stencil9(np.ones((rows, cols, 1)))[..., 0]
    return (D + EPS_DEG) ** -0.5


def setup_inputs():
    s = mx_kscale(IN_DIM)
    mu = 0.5 * np.random.standard_normal(IN_DIM)
    bound = np.sqrt(6.0 / IN_DIM)
    return {"H": bf((np.random.standard_normal((BATCH, N, IN_DIM)) + mu) * s),
            "W": bf(np.random.uniform(-bound, bound, (IN_DIM, OUT_DIM)) / s[:, None]),
            "gamma": bf(1.0 + 0.1 * np.random.standard_normal(OUT_DIM)),
            "beta": bf(0.2 * np.random.standard_normal(OUT_DIM))}


def reference(H, W, gamma, beta):
    B, n_nodes, _ = H.shape
    Ht = mxq(f64(H), 2, "e4m3") @ mxq(f64(W), 0, "e4m3")
    mean = Ht.mean(axis=(0, 1))
    var = Ht.var(axis=(0, 1))
    Ht = (Ht - mean) * (1.0 / np.sqrt(var + EPS_BN)) * f64(gamma) + f64(beta)
    Ht = np.maximum(Ht, 0.0)
    d = _deg_inv_sqrt(ROWS, COLS)[None, :, :, None]
    Hg = Ht.reshape(B, ROWS, COLS, OUT_DIM)
    Hagg = d * _stencil9(Hg * d)
    return Hagg.reshape(B, n_nodes, OUT_DIM)

@@ -1,0 +1,322 @@
+from contextlib import ExitStack
+
+import concourse.mybir as mybir
+from concourse.masks import make_identity
+
+F32 = mybir.dt.float32
+BF16 = mybir.dt.bfloat16
+U32 = mybir.dt.uint32
+U8 = mybir.dt.uint8
+FP8X4 = mybir.dt.float8_e4m3fn_x4
+ACT = mybir.ActivationFunctionType
+ALU = mybir.AluOpType
+AXIS = mybir.AxisListType
+
+P = 128
+BATCH, ROWS, COLS = 2, 64, 64
+IN_DIM, OUT_DIM = 512, 512
+NODES = BATCH * ROWS * COLS
+EPS_BN = 1e-5
+EPS_DEG = 1e-5
+
+PACK = 4
+F_BLOCKS = OUT_DIM // P
+CHUNK_COLS = 4
+CHUNK = CHUNK_COLS * P
+N_CHUNKS = COLS // CHUNK_COLS
+RUNS = CHUNK // ROWS
+HALF = ROWS // 2
+PITCH = 72
+ODD_AT = 4
+EVEN_AT = ODD_AT + HALF
+N_PADDED = 3
+LOAD_BUFS = 6
+AHEAD = 2
+STEP = 2
+LAG = 8
+VECTOR_COLUMN = 1
+
+D9 = (9.0 + EPS_DEG) ** -0.5
+D6 = (6.0 + EPS_DEG) ** -0.5
+D4 = (4.0 + EPS_DEG) ** -0.5
+
+FLOPS = 2 * NODES * IN_DIM * OUT_DIM
+
+
+def column_runs(chunk):
+    if chunk == 0:
+        return [(0, 1, True), (1, CHUNK_COLS - 1, False)]
+    if chunk == N_CHUNKS - 1:
+        return [(0, CHUNK_COLS - 1, False), (CHUNK_COLS - 1, 1, True)]
+    return [(0, CHUNK_COLS, False)]
+
+
+def half_of(count, half):
+    return slice(half * count // 2, (half + 1) * count // 2)
+
+
+def tile_graphconvolutionbatch_kernel(tc, H, W, gamma, beta, out):
+    nc = tc.nc
+    h_view = H.rearrange("b (r c) k -> (b r) c k", c=COLS)
+    out_view = out.rearrange("b (r c) f -> (b r) c f", c=COLS)
+
+    with ExitStack() as ctx:
+        const = ctx.enter_context(tc.tile_pool(name="const", bufs=1))
+        loads = ctx.enter_context(tc.tile_pool(name="loads", bufs=LOAD_BUFS))
+        stage = ctx.enter_context(tc.tile_pool(name="stage", bufs=3))
+        sums = ctx.enter_context(tc.tile_pool(name="sums", bufs=5))
+        halves = ctx.enter_context(tc.tile_pool(name="halves", bufs=2))
+        pairs = ctx.enter_context(tc.tile_pool(name="pairs", bufs=5))
+        stores = ctx.enter_context(tc.tile_pool(name="stores", bufs=3))
+        psum = ctx.enter_context(tc.psum_pool(name="psum", bufs=4))
+
+        h_raw = {}
+
+        def load(chunk):
+            h_raw[chunk] = loads.tile([P, CHUNK_COLS, IN_DIM], BF16, name="h_raw")
+            nc.sync.dma_start(
+                out=h_raw[chunk][:], in_=h_view[:, chunk * CHUNK_COLS : (chunk + 1) * CHUNK_COLS, :]
+            )
+
+        ident = const.tile([P, P], F32)
+        make_identity(nc, ident[:])
+        odd_first = const.tile([P, P], F32)
+        ident_rows = ident[:].rearrange("p (b k t) -> p b t k", b=BATCH, t=2)
+        odd_first_halves = odd_first[:].rearrange("p (b s k) -> p b s k", b=BATCH, s=2)
+        for s in range(2):
+            nc.vector.tensor_copy(out=odd_first_halves[:, :, s, :], in_=ident_rows[:, :, 1 - s, :])
+
+        w_raw = const.tile([P, PACK, OUT_DIM], BF16)
+        nc.sync.dma_start(out=w_raw[:], in_=W.rearrange("(p t) f -> p t f", t=PACK))
+        for chunk in range(LOAD_BUFS):
+            load(chunk)
+        w_grouped = const.tile([P, OUT_DIM, PACK], BF16, align_bytes=64)
+        nc.vector.tensor_copy(out=w_grouped[:], in_=w_raw[:].rearrange("p t f -> p f t"))
+        w_codes = const.tile([P, OUT_DIM], U32, align_bytes=64)
+        w_scales = const.tile([P, OUT_DIM], U8, align_bytes=64)
+        nc.vector.quantize_mx(
+            out=w_codes[:].bitcast(FP8X4),
+            scales=w_scales[:],
+            in_=w_grouped[:].rearrange("p f t -> p (f t)"),
+        )
+
+        gb_rows = const.tile([P, P], BF16)
+        nc.vector.memset(gb_rows[:], 0.0)
+        nc.scalar.dma_start(out=gb_rows[0:F_BLOCKS, :], in_=gamma.rearrange("(j p) -> j p", p=P))
+        nc.scalar.dma_start(
+            out=gb_rows[F_BLOCKS : 2 * F_BLOCKS, :], in_=beta.rearrange("(j p) -> j p", p=P)
+        )
+        gb_rows_f32 = const.tile([P, P], F32)
+        nc.vector.tensor_copy(out=gb_rows_f32[:], in_=gb_rows[:])
+        gb_bank = psum.tile([P, P], F32, tag="t")
+        nc.tensor.transpose(gb_bank[:], gb_rows_f32[:], ident[:])
+        gb = const.tile([P, 2 * F_BLOCKS], F32)
+        nc.vector.tensor_copy(out=gb[:], in_=gb_bank[:, 0 : 2 * F_BLOCKS])
+
+        on_row_edge = const.tile([P, 1], F32)
+        nc.vector.tensor_reduce(
+            out=on_row_edge[:],
+            in_=ident[:].rearrange("p (b r) -> p b r", r=ROWS)[:, :, 0 : ROWS : ROWS - 1],
+            axis=AXIS.XY,
+            op=ALU.add,
+        )
+        rows_in_reach = const.tile([P, 1], F32)
+        nc.vector.tensor_scalar(
+            out=rows_in_reach[:], in0=on_row_edge[:], scalar1=-1.0, scalar2=3.0, op0=ALU.mult, op1=ALU.add
+        )
+        degree = const.tile([P, COLS], F32)
+        nc.vector.memset(degree[:], 3.0)
+        nc.vector.memset(degree[:, 0 : COLS : COLS - 1], 2.0)
+        nc.vector.tensor_scalar(
+            out=degree[:], in0=degree[:], scalar1=rows_in_reach[:, 0:1], scalar2=EPS_DEG, op0=ALU.mult, op1=ALU.add
+        )
+        nc.scalar.sqrt(out=degree[:], in_=degree[:])
+        d_out = const.tile([P, COLS], F32)
+        nc.vector.reciprocal(out=d_out[:], in_=degree[:])
+
+        padded = []
+        for i in range(N_PADDED):
+            pad_tile = const.tile([P, F_BLOCKS * RUNS, PITCH], F32, name="padded%d" % i)
+            nc.vector.memset(pad_tile[:, :, ODD_AT - 1 : ODD_AT + ROWS + 1 : ROWS + 1], 0.0)
+            padded.append(pad_tile)
+
+        h_codes = const.tile([P, NODES], U32, align_bytes=64)
+        h_scales = const.tile([P, NODES], U8, align_bytes=64)
+        stats = const.tile([P, F_BLOCKS, N_CHUNKS, 6], F32)
+
+        def multiply(chunk, fb):
+            nodes = slice(chunk * CHUNK, (chunk + 1) * CHUNK)
+            feats = slice(fb * P, (fb + 1) * P)
+            y = psum.tile([P, CHUNK], F32, tag="y")
+            nc.tensor.matmul_mx(
+                out=y[:],
+                lhsT=w_codes[:, feats].bitcast(FP8X4),
+                lhsT_scale=w_scales[:, feats],
+                rhs=h_codes[:, nodes].bitcast(FP8X4),
+                rhs_scale=h_scales[:, nodes],
+                start=True,
+                stop=True,
+            )
+            return y
+
+        def turn(chunk):
+            grouped = stage.tile([P, CHUNK * PACK], BF16, align_bytes=64, name="grouped")
+            grouped_words = grouped[:].bitcast(F32).rearrange("p (n u) -> p n u", u=2)
+            for half in range(2):
+                turned = psum.tile([P, 2, 2 * P], F32, tag="t", name="turned")
+                for i in range(2):
+                    words = h_raw[chunk][:, 2 * half + i, :].bitcast(F32)
+                    for u in range(2):
+                        nc.tensor.transpose(
+                            turned[:, u, i * P : (i + 1) * P], words[:, u : 2 * P : 2], odd_first[:]
+                        )
+                nc.scalar.copy(
+                    out=grouped_words[:, half * 2 * P : (half + 1) * 2 * P, :],
+                    in_=turned[:].rearrange("p u n -> p n u"),
+                )
+            return grouped
+
+        def quantise(chunk, grouped):
+            nodes = slice(chunk * CHUNK, (chunk + 1) * CHUNK)
+            nc.vector.quantize_mx(
+                out=h_codes[:, nodes].bitcast(FP8X4), scales=h_scales[:, nodes], in_=grouped[:]
+            )
+
+        ctx.enter_context(tc.manual_schedule())
+
+        def prepare(chunk):
+            quantise(chunk, turn(chunk))
+            if chunk + LOAD_BUFS < N_CHUNKS:
+                load(chunk + LOAD_BUFS)
+
+        for chunk in range(AHEAD):
+            prepare(chunk)
+        for chunk in range(N_CHUNKS):
+            for fb in range(F_BLOCKS):
+                y = multiply(chunk, fb)
+                nc.vector.bn_stats(out=stats[:, fb, chunk, :], in_=y[:])
+            if chunk + AHEAD < N_CHUNKS:
+                prepare(chunk + AHEAD)
+
+        mean_var = const.tile([P, F_BLOCKS, 2], F32)
+        for fb in range(F_BLOCKS):
+            nc.vector.bn_aggr(out=mean_var[:, fb, :], in_=stats[:, fb, :, :].rearrange("p j s -> p (j s)"))
+        std = const.tile([P, F_BLOCKS], F32)
+        nc.vector.tensor_scalar_add(out=std[:], in0=mean_var[:, :, 1], scalar1=EPS_BN)
+        nc.scalar.sqrt(out=std[:], in_=std[:])
+        rstd = const.tile([P, F_BLOCKS], F32)
+        nc.vector.reciprocal(out=rstd[:], in_=std[:])
+        gain_shift = const.tile([P, 2, F_BLOCKS], F32)
+        nc.vector.tensor_mul(out=gain_shift[:, 0, :], in0=gb[:, 0:F_BLOCKS], in1=rstd[:])
+        mean_gain = const.tile([P, F_BLOCKS], F32)
+        nc.vector.tensor_mul(out=mean_gain[:], in0=mean_var[:, :, 0], in1=gain_shift[:, 0, :])
+        nc.vector.tensor_sub(out=gain_shift[:, 1, :], in0=gb[:, F_BLOCKS : 2 * F_BLOCKS], in1=mean_gain[:])
+        inner = const.tile([P, 2, F_BLOCKS], F32)
+        nc.vector.tensor_scalar_mul(out=inner[:], in0=gain_shift[:], scalar1=D9)
+        edge = const.tile([P, 2, F_BLOCKS], F32)
+        nc.vector.tensor_scalar_mul(out=edge[:], in0=gain_shift[:], scalar1=D6)
+
+        row_sums = {}
+        pair_sums = {}
+        results = {}
+
+        def norm_relu(chunk, fb):
+            pad_tile = padded[chunk % N_PADDED]
+            y = multiply(chunk, fb)
+            y_runs = y[:].rearrange("p (q r) -> p q r", r=ROWS)
+            for first, count, on_edge in column_runs(chunk):
+                coeff = edge if on_edge else inner
+                nc.scalar.activation(
+                    out=pad_tile[:, fb * RUNS + BATCH * first : fb * RUNS + BATCH * (first + count), ODD_AT : ODD_AT + ROWS],
+                    in_=y_runs[:, BATCH * first : BATCH * (first + count), :],
+                    func=ACT.Relu,
+                    bias=coeff[:, 1, fb : fb + 1],
+                    scale=coeff[:, 0, fb : fb + 1],
+                )
+
+        def sum_over_rows(chunk):
+            pad_tile = padded[chunk % N_PADDED]
+            n_runs = F_BLOCKS * RUNS
+            by_block = pad_tile[:].rearrange("p (f q) s -> p f q s", f=F_BLOCKS)
+            for half in range(2):
+                for first, count, on_edge in column_runs(chunk):
+                    ends = by_block[
+                        :, half_of(F_BLOCKS, half), BATCH * first : BATCH * (first + count), EVEN_AT - 1 : EVEN_AT + 1
+                    ]
+                    nc.vector.tensor_scalar_mul(out=ends, in0=ends, scalar1=(D4 / D6 if on_edge else D6 / D9))
+            both = halves.tile([P, n_runs, HALF], F32, name="both")
+            for half in range(2):
+                runs = half_of(n_runs, half)
+                nc.vector.tensor_add(
+                    out=both[:, runs, :],
+                    in0=pad_tile[:, runs, EVEN_AT : EVEN_AT + HALF],
+                    in1=pad_tile[:, runs, ODD_AT : ODD_AT + HALF],
+                )
+            outer = (
+                pad_tile[:, :, ODD_AT - 1 : ODD_AT - 1 + 2 * (HALF + 2)]
+                .rearrange("p g (t w) -> p g t w", t=2)[:, :, :, 0:HALF]
+                .rearrange("p g t k -> p g k t")
+            )
+            total = sums.tile([P, F_BLOCKS, CHUNK], F32, name="total")
+            total_runs = total[:].rearrange("p f (q k t) -> p (f q) k t", k=HALF, t=2)
+            for half in range(2):
+                runs = half_of(n_runs, half)
+                nc.vector.tensor_add(
+                    out=total_runs[:, runs, :, :],
+                    in0=both[:, runs, :].unsqueeze(3).to_broadcast([P, n_runs // 2, HALF, 2]),
+                    in1=outer[:, runs, :, :],
+                )
+            row_sums[chunk] = total
+            pair = pairs.tile([P, F_BLOCKS, CHUNK // 2], F32, name="pair")
+            pair_columns = pair[:].rearrange("p f (e n) -> p (f e) n", n=P)
+            columns = total[:].rearrange("p f (e two n) -> p (f e) two n", two=2, n=P)
+            for half in range(2):
+                some = half_of(F_BLOCKS * CHUNK_COLS // 2, half)
+                nc.vector.tensor_add(
+                    out=pair_columns[:, some, :], in0=columns[:, some, 0, :], in1=columns[:, some, 1, :]
+                )
+            pair_sums[chunk] = pair
+
+        def finish_column(c):
+            beyond = c - 1 if c % 2 == 0 else c + 1
+            parts = [(pair_sums[c // CHUNK_COLS], (c % CHUNK_COLS) // 2)]
+            if 0 <= beyond < COLS:
+                parts.append((row_sums[beyond // CHUNK_COLS], beyond % CHUNK_COLS))
+            turned_back = psum.tile([P, OUT_DIM], F32, tag="t")
+            for i, (source, col) in enumerate(parts):
+                for fb in range(F_BLOCKS):
+                    nc.tensor.matmul(
+                        out=turned_back[:, fb * P : (fb + 1) * P],
+                        lhsT=source[:, fb, col * P : (col + 1) * P],
+                        rhs=ident[:],
+                        is_transpose=True,
+                        start=(i == 0 and fb == 0),
+                        stop=(i == len(parts) - 1 and fb == F_BLOCKS - 1),
+                    )
+            group = c // CHUNK_COLS
+            if c % CHUNK_COLS == 0:
+                results[group] = stores.tile([P, CHUNK_COLS, OUT_DIM], F32, name="result")
+            if c % CHUNK_COLS == VECTOR_COLUMN:
+                nc.vector.tensor_scalar_mul(
+                    out=results[group][:, c % CHUNK_COLS, :], in0=turned_back[:], scalar1=d_out[:, c : c + 1]
+                )
+            else:
+                nc.scalar.activation(
+                    out=results[group][:, c % CHUNK_COLS, :],
+                    in_=turned_back[:],
+                    func=ACT.Copy,
+                    scale=d_out[:, c : c + 1],
+                )
+            if c % CHUNK_COLS == CHUNK_COLS - 1:
+                nc.sync.dma_start(
+                    out=out_view[:, group * CHUNK_COLS : (group + 1) * CHUNK_COLS, :], in_=results[group][:]
+                )
+
+        n_passes = N_CHUNKS * F_BLOCKS
+        for first_pass in range(0, n_passes + LAG, STEP):
+            for m in range(first_pass, min(first_pass + STEP, n_passes)):
+                norm_relu(m // F_BLOCKS, m % F_BLOCKS)
+                if m % F_BLOCKS == F_BLOCKS - 1:
+                    sum_over_rows(m // F_BLOCKS)
+            for c in range(max(first_pass - LAG, 0), min(first_pass - LAG + STEP, COLS)):
+                finish_column(c)

@@ -24,17 +24,19 @@ F_BLOCKS = OUT_DIM // P
 CHUNK_COLS = 4
 CHUNK = CHUNK_COLS * P
 N_CHUNKS = COLS // CHUNK_COLS
-RUNS = CHUNK // ROWS
-HALF = ROWS // 2
-PITCH = 72
-ODD_AT = 4
-EVEN_AT = ODD_AT + HALF
-N_PADDED = 3
+ROW_PAIRS = ROWS // 2
+PITCH = P + 4
+RUN_AT = 4
+HALF = CHUNK // 2
+ODD_AT = HALF + 8
+SPLIT = 2 * ODD_AT
+N_PADDED = 4
+VECTOR_BLOCKS = 2
+TENSOR_BLOCKS = F_BLOCKS - VECTOR_BLOCKS
+KEPT = F_BLOCKS - 1
 LOAD_BUFS = 6
 AHEAD = 2
-STEP = 2
-LAG = 8
-VECTOR_COLUMN = 1
+LAG = 2
 
 D9 = (9.0 + EPS_DEG) ** -0.5
 D6 = (6.0 + EPS_DEG) ** -0.5
@@ -51,103 +53,130 @@ def column_runs(chunk):
     return [(0, CHUNK_COLS, False)]
 
 
-def half_of(count, half):
-    return slice(half * count // 2, (half + 1) * count // 2)
-
-
 def tile_graphconvolutionbatch_kernel(tc, H, W, gamma, beta, out):
     nc = tc.nc
     h_view = H.rearrange("b (r c) k -> (b r) c k", c=COLS)
-    out_view = out.rearrange("b (r c) f -> (b r) c f", c=COLS)
+    out_view = out.rearrange("b (r c) f -> b r c f", c=COLS)
 
     with ExitStack() as ctx:
         const = ctx.enter_context(tc.tile_pool(name="const", bufs=1))
         loads = ctx.enter_context(tc.tile_pool(name="loads", bufs=LOAD_BUFS))
         stage = ctx.enter_context(tc.tile_pool(name="stage", bufs=3))
-        sums = ctx.enter_context(tc.tile_pool(name="sums", bufs=5))
+        sums = ctx.enter_context(tc.tile_pool(name="sums", bufs=3))
         halves = ctx.enter_context(tc.tile_pool(name="halves", bufs=2))
-        pairs = ctx.enter_context(tc.tile_pool(name="pairs", bufs=5))
+        columns = ctx.enter_context(tc.tile_pool(name="columns", bufs=4))
         stores = ctx.enter_context(tc.tile_pool(name="stores", bufs=3))
-        psum = ctx.enter_context(tc.psum_pool(name="psum", bufs=4))
+        psum_y = ctx.enter_context(tc.psum_pool(name="psum_y", bufs=4))
+        psum_t = ctx.enter_context(tc.psum_pool(name="psum_t", bufs=4))
 
         h_raw = {}
 
         def load(chunk):
             h_raw[chunk] = loads.tile([P, CHUNK_COLS, IN_DIM], BF16, name="h_raw")
+            load_columns(chunk, 0, CHUNK_COLS)
+
+        def load_columns(chunk, first, last):
             nc.sync.dma_start(
-                out=h_raw[chunk][:], in_=h_view[:, chunk * CHUNK_COLS : (chunk + 1) * CHUNK_COLS, :]
+                out=h_raw[chunk][:, first:last, :],
+                in_=h_view[:, chunk * CHUNK_COLS + first : chunk * CHUNK_COLS + last, :],
             )
 
-        ident = const.tile([P, P], F32)
-        make_identity(nc, ident[:])
-        odd_first = const.tile([P, P], F32)
-        ident_rows = ident[:].rearrange("p (b k t) -> p b t k", b=BATCH, t=2)
-        odd_first_halves = odd_first[:].rearrange("p (b s k) -> p b s k", b=BATCH, s=2)
-        for s in range(2):
-            nc.vector.tensor_copy(out=odd_first_halves[:, :, s, :], in_=ident_rows[:, :, 1 - s, :])
+        ctx.enter_context(tc.manual_schedule())
 
+        h_raw[0] = loads.tile([P, CHUNK_COLS, IN_DIM], BF16, name="h_raw")
+        load_columns(0, 0, CHUNK_COLS // 2)
         w_raw = const.tile([P, PACK, OUT_DIM], BF16)
         nc.sync.dma_start(out=w_raw[:], in_=W.rearrange("(p t) f -> p t f", t=PACK))
-        for chunk in range(LOAD_BUFS):
+        load_columns(0, CHUNK_COLS // 2, CHUNK_COLS)
+        for chunk in range(1, LOAD_BUFS):
             load(chunk)
-        w_grouped = const.tile([P, OUT_DIM, PACK], BF16, align_bytes=64)
-        nc.vector.tensor_copy(out=w_grouped[:], in_=w_raw[:].rearrange("p t f -> p f t"))
-        w_codes = const.tile([P, OUT_DIM], U32, align_bytes=64)
-        w_scales = const.tile([P, OUT_DIM], U8, align_bytes=64)
-        nc.vector.quantize_mx(
-            out=w_codes[:].bitcast(FP8X4),
-            scales=w_scales[:],
-            in_=w_grouped[:].rearrange("p f t -> p (f t)"),
-        )
-
         gb_rows = const.tile([P, P], BF16)
         nc.vector.memset(gb_rows[:], 0.0)
         nc.scalar.dma_start(out=gb_rows[0:F_BLOCKS, :], in_=gamma.rearrange("(j p) -> j p", p=P))
         nc.scalar.dma_start(
             out=gb_rows[F_BLOCKS : 2 * F_BLOCKS, :], in_=beta.rearrange("(j p) -> j p", p=P)
         )
+        one = const.tile([P, 1], F32)
+        nc.vector.memset(one[:], 1.0)
+        nc.scalar.sqrt(out=one[:], in_=one[:])
+
+        ident = const.tile([P, P], F32)
+        make_identity(nc, ident[:])
+        by_row = const.tile([P, P], F32)
+        nc.vector.tensor_copy(
+            out=by_row[:].rearrange("p (r b) -> p b r", b=BATCH),
+            in_=ident[:].rearrange("p (b r) -> p b r", b=BATCH),
+        )
+
+        w_grouped = const.tile([P, OUT_DIM, PACK], BF16, align_bytes=64)
+        w_codes = const.tile([P, OUT_DIM], U32, align_bytes=64)
+        w_scales = const.tile([P, OUT_DIM], U8, align_bytes=64)
         gb_rows_f32 = const.tile([P, P], F32)
-        nc.vector.tensor_copy(out=gb_rows_f32[:], in_=gb_rows[:])
-        gb_bank = psum.tile([P, P], F32, tag="t")
-        nc.tensor.transpose(gb_bank[:], gb_rows_f32[:], ident[:])
-        gb = const.tile([P, 2 * F_BLOCKS], F32)
-        nc.vector.tensor_copy(out=gb[:], in_=gb_bank[:, 0 : 2 * F_BLOCKS])
+        gb = const.tile([P, 2, 2, F_BLOCKS], F32)
+
+        def quantise_weights():
+            nc.vector.tensor_copy(out=w_grouped[:], in_=w_raw[:].rearrange("p t f -> p f t"))
+            nc.vector.quantize_mx(
+                out=w_codes[:].bitcast(FP8X4),
+                scales=w_scales[:],
+                in_=w_grouped[:].rearrange("p f t -> p (f t)"),
+            )
+
+        def turn_gamma_beta():
+            bank = psum_t.tile([P, P], F32, tag="t", name="gb_bank")
+            nc.tensor.transpose(bank[:], gb_rows_f32[:], ident[:])
+            for i, factor in enumerate((D9 * D9, D6 * D9)):
+                nc.vector.tensor_scalar_mul(
+                    out=gb[:, i, :, :],
+                    in0=bank[:, 0 : 2 * F_BLOCKS].rearrange("p (s f) -> p s f", s=2),
+                    scalar1=factor,
+                )
 
         on_row_edge = const.tile([P, 1], F32)
         nc.vector.tensor_reduce(
             out=on_row_edge[:],
-            in_=ident[:].rearrange("p (b r) -> p b r", r=ROWS)[:, :, 0 : ROWS : ROWS - 1],
+            in_=ident[:].rearrange("p (r b) -> p r b", b=BATCH)[:, 0 : ROWS : ROWS - 1, :],
             axis=AXIS.XY,
             op=ALU.add,
         )
-        rows_in_reach = const.tile([P, 1], F32)
+        row_factor = const.tile([P, 1], F32)
         nc.vector.tensor_scalar(
-            out=rows_in_reach[:], in0=on_row_edge[:], scalar1=-1.0, scalar2=3.0, op0=ALU.mult, op1=ALU.add
+            out=row_factor[:], in0=on_row_edge[:], scalar1=D6 / D9 - 1.0, scalar2=1.0, op0=ALU.mult, op1=ALU.add
         )
-        degree = const.tile([P, COLS], F32)
-        nc.vector.memset(degree[:], 3.0)
-        nc.vector.memset(degree[:, 0 : COLS : COLS - 1], 2.0)
+        column_factor = const.tile([P, 1], F32)
         nc.vector.tensor_scalar(
-            out=degree[:], in0=degree[:], scalar1=rows_in_reach[:, 0:1], scalar2=EPS_DEG, op0=ALU.mult, op1=ALU.add
+            out=column_factor[:],
+            in0=on_row_edge[:],
+            scalar1=D4 / D6 - D6 / D9,
+            scalar2=D6 / D9,
+            op0=ALU.mult,
+            op1=ALU.add,
         )
-        nc.scalar.sqrt(out=degree[:], in_=degree[:])
-        d_out = const.tile([P, COLS], F32)
-        nc.vector.reciprocal(out=d_out[:], in_=degree[:])
 
+        n_runs = TENSOR_BLOCKS * CHUNK_COLS
         padded = []
+        split = []
         for i in range(N_PADDED):
-            pad_tile = const.tile([P, F_BLOCKS * RUNS, PITCH], F32, name="padded%d" % i)
-            nc.vector.memset(pad_tile[:, :, ODD_AT - 1 : ODD_AT + ROWS + 1 : ROWS + 1], 0.0)
+            pad_tile = const.tile([P, (n_runs + 1) * PITCH], F32, name="padded%d" % i)
+            nc.gpsimd.memset(pad_tile[:].rearrange("p (g s) -> p g s", s=PITCH)[:, :, 0:RUN_AT], 0.0)
             padded.append(pad_tile)
+            split_tile = const.tile([P, VECTOR_BLOCKS * SPLIT + P], F32, name="split%d" % i)
+            gaps = split_tile[:, 0 : VECTOR_BLOCKS * SPLIT].rearrange("p (g w) -> p g w", w=ODD_AT)[:, :, HALF:ODD_AT]
+            nc.gpsimd.memset(gaps, 0.0)
+            split.append(split_tile)
 
         h_codes = const.tile([P, NODES], U32, align_bytes=64)
         h_scales = const.tile([P, NODES], U8, align_bytes=64)
-        stats = const.tile([P, F_BLOCKS, N_CHUNKS, 6], F32)
+        stats = const.tile([P, KEPT, N_CHUNKS, 6], F32)
+        y_kept = const.tile([P, NODES], F32)
+        kept_sums = const.tile([P, 2, N_CHUNKS], F32)
+        minus_first = const.tile([P, 1], F32)
+        squares = const.tile([P, CHUNK], F32)
 
         def multiply(chunk, fb):
             nodes = slice(chunk * CHUNK, (chunk + 1) * CHUNK)
             feats = slice(fb * P, (fb + 1) * P)
-            y = psum.tile([P, CHUNK], F32, tag="y")
+            y = psum_y.tile([P, CHUNK], F32, tag="y")
             nc.tensor.matmul_mx(
                 out=y[:],
                 lhsT=w_codes[:, feats].bitcast(FP8X4),
@@ -163,12 +192,12 @@ def tile_graphconvolutionbatch_kernel(tc, H, W, gamma, beta, out):
             grouped = stage.tile([P, CHUNK * PACK], BF16, align_bytes=64, name="grouped")
             grouped_words = grouped[:].bitcast(F32).rearrange("p (n u) -> p n u", u=2)
             for half in range(2):
-                turned = psum.tile([P, 2, 2 * P], F32, tag="t", name="turned")
+                turned = psum_t.tile([P, 2, 2 * P], F32, tag="t", name="turned")
                 for i in range(2):
                     words = h_raw[chunk][:, 2 * half + i, :].bitcast(F32)
                     for u in range(2):
                         nc.tensor.transpose(
-                            turned[:, u, i * P : (i + 1) * P], words[:, u : 2 * P : 2], odd_first[:]
+                            turned[:, u, i * P : (i + 1) * P], words[:, u : 2 * P : 2], by_row[:]
                         )
                 nc.scalar.copy(
                     out=grouped_words[:, half * 2 * P : (half + 1) * 2 * P, :],
@@ -182,141 +211,262 @@ def tile_graphconvolutionbatch_kernel(tc, H, W, gamma, beta, out):
                 out=h_codes[:, nodes].bitcast(FP8X4), scales=h_scales[:, nodes], in_=grouped[:]
             )
 
-        ctx.enter_context(tc.manual_schedule())
+        def keep(chunk, y):
+            nodes = slice(chunk * CHUNK, (chunk + 1) * CHUNK)
+            nc.scalar.activation(
+                out=y_kept[:, nodes], in_=y[:], func=ACT.Identity, accum_out=kept_sums[:, 0, chunk : chunk + 1]
+            )
+            if chunk == 0:
+                nc.scalar.mul(out=minus_first[:], in_=kept_sums[:, 0, 0:1], mul=-1.0 / CHUNK)
 
-        def prepare(chunk):
-            quantise(chunk, turn(chunk))
-            if chunk + LOAD_BUFS < N_CHUNKS:
-                load(chunk + LOAD_BUFS)
+        def square(chunk):
+            nodes = slice(chunk * CHUNK, (chunk + 1) * CHUNK)
+            nc.scalar.activation(
+                out=squares[:],
+                in_=y_kept[:, nodes],
+                func=ACT.Square,
+                bias=minus_first[:, 0:1],
+                accum_out=kept_sums[:, 1, chunk : chunk + 1],
+            )
 
+        groups = {}
         for chunk in range(AHEAD):
-            prepare(chunk)
+            groups[chunk] = turn(chunk)
+            if chunk == 0:
+                quantise_weights()
+            quantise(chunk, groups[chunk])
+            load(chunk + LOAD_BUFS)
         for chunk in range(N_CHUNKS):
-            for fb in range(F_BLOCKS):
-                y = multiply(chunk, fb)
-                nc.vector.bn_stats(out=stats[:, fb, chunk, :], in_=y[:])
-            if chunk + AHEAD < N_CHUNKS:
-                prepare(chunk + AHEAD)
+            ahead = chunk + AHEAD
+            keep(chunk, multiply(chunk, KEPT))
+            ys = [multiply(chunk, fb) for fb in range(KEPT)]
+            for fb in range(KEPT):
+                nc.vector.bn_stats(out=stats[:, fb, chunk, :], in_=ys[fb][:])
+            if ahead < N_CHUNKS:
+                quantise(ahead, turn(ahead))
+                if ahead + LOAD_BUFS < N_CHUNKS:
+                    load(ahead + LOAD_BUFS)
+            if chunk > 0:
+                square(chunk - 1)
+            if chunk == AHEAD:
+                nc.vector.tensor_copy(out=gb_rows_f32[:], in_=gb_rows[:])
+            if chunk == AHEAD + 1:
+                turn_gamma_beta()
+        square(N_CHUNKS - 1)
 
         mean_var = const.tile([P, F_BLOCKS, 2], F32)
-        for fb in range(F_BLOCKS):
+        kept_totals = const.tile([P, 2], F32)
+        off_first = const.tile([P, 2], F32)
+
+        def aggregate(fb):
             nc.vector.bn_aggr(out=mean_var[:, fb, :], in_=stats[:, fb, :, :].rearrange("p j s -> p (j s)"))
+
+        aggregate(0)
+        nc.vector.tensor_reduce(out=kept_totals[:], in_=kept_sums[:], axis=AXIS.X, op=ALU.add)
+        aggregate(1)
+        nc.vector.tensor_scalar_mul(out=mean_var[:, KEPT, :], in0=kept_totals[:], scalar1=1.0 / NODES)
+        nc.vector.tensor_scalar(
+            out=off_first[:, 0:1], in0=kept_totals[:, 0:1], scalar1=1.0 / NODES, scalar2=minus_first[:, 0:1],
+            op0=ALU.mult, op1=ALU.add,
+        )
+        aggregate(2)
+        nc.vector.tensor_mul(out=off_first[:, 1:2], in0=off_first[:, 0:1], in1=off_first[:, 0:1])
+        nc.vector.tensor_sub(out=mean_var[:, KEPT, 1:2], in0=mean_var[:, KEPT, 1:2], in1=off_first[:, 1:2])
         std = const.tile([P, F_BLOCKS], F32)
         nc.vector.tensor_scalar_add(out=std[:], in0=mean_var[:, :, 1], scalar1=EPS_BN)
         nc.scalar.sqrt(out=std[:], in_=std[:])
         rstd = const.tile([P, F_BLOCKS], F32)
         nc.vector.reciprocal(out=rstd[:], in_=std[:])
-        gain_shift = const.tile([P, 2, F_BLOCKS], F32)
-        nc.vector.tensor_mul(out=gain_shift[:, 0, :], in0=gb[:, 0:F_BLOCKS], in1=rstd[:])
-        mean_gain = const.tile([P, F_BLOCKS], F32)
-        nc.vector.tensor_mul(out=mean_gain[:], in0=mean_var[:, :, 0], in1=gain_shift[:, 0, :])
-        nc.vector.tensor_sub(out=gain_shift[:, 1, :], in0=gb[:, F_BLOCKS : 2 * F_BLOCKS], in1=mean_gain[:])
-        inner = const.tile([P, 2, F_BLOCKS], F32)
-        nc.vector.tensor_scalar_mul(out=inner[:], in0=gain_shift[:], scalar1=D9)
-        edge = const.tile([P, 2, F_BLOCKS], F32)
-        nc.vector.tensor_scalar_mul(out=edge[:], in0=gain_shift[:], scalar1=D6)
+        coeffs = const.tile([P, 2, 2, F_BLOCKS], F32)
+        mean_gain = const.tile([P, 2, F_BLOCKS], F32)
+        wide = [P, 2, F_BLOCKS]
+        nc.vector.tensor_mul(
+            out=coeffs[:, :, 0, :], in0=gb[:, :, 0, :], in1=rstd[:].unsqueeze(1).to_broadcast(wide)
+        )
+        nc.vector.tensor_mul(
+            out=mean_gain[:], in0=coeffs[:, :, 0, :], in1=mean_var[:, :, 0].unsqueeze(1).to_broadcast(wide)
+        )
+        nc.vector.tensor_sub(out=coeffs[:, :, 1, :], in0=gb[:, :, 1, :], in1=mean_gain[:])
 
         row_sums = {}
-        pair_sums = {}
+        evens = {}
+        boths = {}
+        banks = {}
         results = {}
 
-        def norm_relu(chunk, fb):
-            pad_tile = padded[chunk % N_PADDED]
-            y = multiply(chunk, fb)
-            y_runs = y[:].rearrange("p (q r) -> p q r", r=ROWS)
+        def norm_relu(chunk, fb, y):
             for first, count, on_edge in column_runs(chunk):
-                coeff = edge if on_edge else inner
+                coeff = coeffs[:, 1 if on_edge else 0, :, :]
+                if fb < TENSOR_BLOCKS:
+                    at = fb * CHUNK_COLS + first
+                    runs = padded[chunk % N_PADDED][:].rearrange("p (g s) -> p g s", s=PITCH)
+                    z_out = runs[:, at : at + count, RUN_AT:PITCH]
+                    y_in = y.rearrange("p (q n) -> p q n", n=P)[:, first : first + count, :]
+                else:
+                    at = (fb - TENSOR_BLOCKS) * SPLIT
+                    by_parity = split[chunk % N_PADDED][:, at : at + SPLIT].rearrange("p (t m b) -> p t m b", t=2, b=BATCH)
+                    pairs = slice(first * ROW_PAIRS, (first + count) * ROW_PAIRS)
+                    z_out = by_parity[:, :, pairs, :]
+                    y_in = y.rearrange("p (m t b) -> p t m b", t=2, b=BATCH)[:, :, pairs, :]
                 nc.scalar.activation(
-                    out=pad_tile[:, fb * RUNS + BATCH * first : fb * RUNS + BATCH * (first + count), ODD_AT : ODD_AT + ROWS],
-                    in_=y_runs[:, BATCH * first : BATCH * (first + count), :],
+                    out=z_out,
+                    in_=y_in,
                     func=ACT.Relu,
                     bias=coeff[:, 1, fb : fb + 1],
                     scale=coeff[:, 0, fb : fb + 1],
                 )
 
-        def sum_over_rows(chunk):
-            pad_tile = padded[chunk % N_PADDED]
-            n_runs = F_BLOCKS * RUNS
-            by_block = pad_tile[:].rearrange("p (f q) s -> p f q s", f=F_BLOCKS)
-            for half in range(2):
-                for first, count, on_edge in column_runs(chunk):
-                    ends = by_block[
-                        :, half_of(F_BLOCKS, half), BATCH * first : BATCH * (first + count), EVEN_AT - 1 : EVEN_AT + 1
-                    ]
-                    nc.vector.tensor_scalar_mul(out=ends, in0=ends, scalar1=(D4 / D6 if on_edge else D6 / D9))
-            both = halves.tile([P, n_runs, HALF], F32, name="both")
-            for half in range(2):
-                runs = half_of(n_runs, half)
-                nc.vector.tensor_add(
-                    out=both[:, runs, :],
-                    in0=pad_tile[:, runs, EVEN_AT : EVEN_AT + HALF],
-                    in1=pad_tile[:, runs, ODD_AT : ODD_AT + HALF],
+        def scale_row_ends_padded(chunk):
+            runs = padded[chunk % N_PADDED][:].rearrange("p (g s) -> p g s", s=PITCH)
+            n_runs = TENSOR_BLOCKS * CHUNK_COLS
+
+            def scale(some, factor):
+                ends = some[:, :, RUN_AT:PITCH].rearrange("p g (r b) -> p g r b", b=BATCH)[:, :, 0 : ROWS : ROWS - 1, :]
+                nc.scalar.mul(out=ends, in_=ends, mul=factor)
+
+            scale(runs[:, 0:n_runs, :], D6 / D9)
+            for first, count, on_edge in column_runs(chunk):
+                if on_edge:
+                    scale(runs[:, first : n_runs : CHUNK_COLS, :], (D4 / D6) / (D6 / D9))
+
+        def scale_row_ends_split(chunk):
+            apart = ODD_AT + P // 2 - BATCH
+            for i in range(VECTOR_BLOCKS):
+                ends = (
+                    split[chunk % N_PADDED][:, i * SPLIT : i * SPLIT + 2 * apart]
+                    .rearrange("p (t w) -> p t w", t=2)[:, :, 0:HALF]
+                    .rearrange("p t (q n) -> p t q n", q=CHUNK_COLS)[:, :, :, 0:BATCH]
                 )
-            outer = (
-                pad_tile[:, :, ODD_AT - 1 : ODD_AT - 1 + 2 * (HALF + 2)]
-                .rearrange("p g (t w) -> p g t w", t=2)[:, :, :, 0:HALF]
-                .rearrange("p g t k -> p g k t")
-            )
-            total = sums.tile([P, F_BLOCKS, CHUNK], F32, name="total")
-            total_runs = total[:].rearrange("p f (q k t) -> p (f q) k t", k=HALF, t=2)
-            for half in range(2):
-                runs = half_of(n_runs, half)
+                for first, count, on_edge in column_runs(chunk):
+                    some = ends[:, :, first : first + count, :]
+                    nc.scalar.mul(out=some, in_=some, mul=D4 / D6 if on_edge else D6 / D9)
+
+        both_rows = {}
+
+        def sum_over_rows(chunk):
+            z = split[chunk % N_PADDED]
+            both = halves.tile([P, VECTOR_BLOCKS, HALF], F32, name="both_rows")
+            total = sums.tile([P, VECTOR_BLOCKS, CHUNK], F32, name="total")
+            for i in range(VECTOR_BLOCKS):
+                at = i * SPLIT
                 nc.vector.tensor_add(
-                    out=total_runs[:, runs, :, :],
-                    in0=both[:, runs, :].unsqueeze(3).to_broadcast([P, n_runs // 2, HALF, 2]),
-                    in1=outer[:, runs, :, :],
+                    out=both[:, i, :], in0=z[:, at : at + HALF], in1=z[:, at + ODD_AT : at + ODD_AT + HALF]
+                )
+            for i in range(VECTOR_BLOCKS):
+                at = i * SPLIT + BATCH
+                outer = (
+                    z[:, at : at + 2 * (ODD_AT - 2 * BATCH)]
+                    .rearrange("p (t w) -> p t w", t=2)[:, ::-1, 0:HALF]
+                    .rearrange("p t (m b) -> p m t b", b=BATCH)
+                )
+                nc.vector.tensor_add(
+                    out=total[:, i, :].rearrange("p (m t b) -> p m t b", t=2, b=BATCH),
+                    in0=both[:, i, :].rearrange("p (m b) -> p m b", b=BATCH).unsqueeze(2).to_broadcast([P, HALF // BATCH, 2, BATCH]),
+                    in1=outer,
                 )
             row_sums[chunk] = total
-            pair = pairs.tile([P, F_BLOCKS, CHUNK // 2], F32, name="pair")
-            pair_columns = pair[:].rearrange("p f (e n) -> p (f e) n", n=P)
-            columns = total[:].rearrange("p f (e two n) -> p (f e) two n", two=2, n=P)
-            for half in range(2):
-                some = half_of(F_BLOCKS * CHUNK_COLS // 2, half)
-                nc.vector.tensor_add(
-                    out=pair_columns[:, some, :], in0=columns[:, some, 0, :], in1=columns[:, some, 1, :]
-                )
-            pair_sums[chunk] = pair
+            both_rows[chunk] = both
 
-        def finish_column(c):
-            beyond = c - 1 if c % 2 == 0 else c + 1
-            parts = [(pair_sums[c // CHUNK_COLS], (c % CHUNK_COLS) // 2)]
-            if 0 <= beyond < COLS:
-                parts.append((row_sums[beyond // CHUNK_COLS], beyond % CHUNK_COLS))
-            turned_back = psum.tile([P, OUT_DIM], F32, tag="t")
-            for i, (source, col) in enumerate(parts):
-                for fb in range(F_BLOCKS):
-                    nc.tensor.matmul(
-                        out=turned_back[:, fb * P : (fb + 1) * P],
-                        lhsT=source[:, fb, col * P : (col + 1) * P],
-                        rhs=ident[:],
-                        is_transpose=True,
-                        start=(i == 0 and fb == 0),
-                        stop=(i == len(parts) - 1 and fb == F_BLOCKS - 1),
-                    )
+        def mend_row_ends(chunk):
+            ends = row_sums[chunk][:].rearrange("p i (q n) -> p (i q) n", n=P)
+            ends = ends.rearrange("p g (r b) -> p g r b", b=BATCH)[:, :, 0 : ROWS : ROWS - 1, :]
+            pairs = both_rows[chunk][:].rearrange("p i (q n) -> p (i q) n", q=CHUNK_COLS)
+            pairs = pairs.rearrange("p g (k b) -> p g k b", b=BATCH)[:, :, 0 : ROW_PAIRS : ROW_PAIRS - 1, :]
+            nc.vector.tensor_copy(out=ends, in_=pairs)
+
+        def turn_back(c):
+            chunk, col = c // CHUNK_COLS, c % CHUNK_COLS
+            pad_tile = padded[chunk % N_PADDED]
+            parts = []
+            for fb in range(TENSOR_BLOCKS):
+                at = (fb * CHUNK_COLS + col) * PITCH + RUN_AT
+                for shift in (-BATCH, 0, BATCH):
+                    parts.append((fb, pad_tile[:, at + shift : at + shift + P]))
+            for i in range(VECTOR_BLOCKS):
+                parts.append((TENSOR_BLOCKS + i, row_sums[chunk][:, i, col * P : (col + 1) * P]))
+            bank = psum_t.tile([P, OUT_DIM], F32, tag="t", name="bank")
+            for i, (fb, source) in enumerate(parts):
+                nc.tensor.matmul(
+                    out=bank[:, fb * P : (fb + 1) * P],
+                    lhsT=source,
+                    rhs=ident[:],
+                    is_transpose=True,
+                    start=(i == 0),
+                    stop=(i == len(parts) - 1),
+                )
+            banks[c] = bank
+
+        def result_of(c):
             group = c // CHUNK_COLS
-            if c % CHUNK_COLS == 0:
+            if group not in results:
                 results[group] = stores.tile([P, CHUNK_COLS, OUT_DIM], F32, name="result")
-            if c % CHUNK_COLS == VECTOR_COLUMN:
-                nc.vector.tensor_scalar_mul(
-                    out=results[group][:, c % CHUNK_COLS, :], in0=turned_back[:], scalar1=d_out[:, c : c + 1]
-                )
-            else:
-                nc.scalar.activation(
-                    out=results[group][:, c % CHUNK_COLS, :],
-                    in_=turned_back[:],
-                    func=ACT.Copy,
-                    scale=d_out[:, c : c + 1],
-                )
-            if c % CHUNK_COLS == CHUNK_COLS - 1:
+            return results[group][:, c % CHUNK_COLS, :]
+
+        def store(group):
+            for b in range(BATCH):
                 nc.sync.dma_start(
-                    out=out_view[:, group * CHUNK_COLS : (group + 1) * CHUNK_COLS, :], in_=results[group][:]
+                    out=out_view[b, :, group * CHUNK_COLS : (group + 1) * CHUNK_COLS, :],
+                    in_=results[group][b : P : BATCH, :, :],
                 )
 
-        n_passes = N_CHUNKS * F_BLOCKS
-        for first_pass in range(0, n_passes + LAG, STEP):
-            for m in range(first_pass, min(first_pass + STEP, n_passes)):
-                norm_relu(m // F_BLOCKS, m % F_BLOCKS)
-                if m % F_BLOCKS == F_BLOCKS - 1:
-                    sum_over_rows(m // F_BLOCKS)
-            for c in range(max(first_pass - LAG, 0), min(first_pass - LAG + STEP, COLS)):
-                finish_column(c)
+        def take_even(e):
+            evens[e] = columns.tile([P, OUT_DIM], F32, name="even")
+            nc.scalar.activation(out=evens[e][:], in_=banks[2 * e][:], func=ACT.Copy, scale=row_factor[:, 0:1])
+
+        def add_pair(e):
+            boths[e] = columns.tile([P, OUT_DIM], F32, name="both_columns")
+            nc.vector.scalar_tensor_tensor(
+                out=boths[e][:], in0=banks[2 * e + 1][:], scalar=row_factor[:, 0:1], in1=evens[e][:],
+                op0=ALU.mult, op1=ALU.add,
+            )
+
+        def finish_even(e):
+            if e == 0:
+                nc.vector.tensor_scalar_mul(out=result_of(0), in0=boths[0][:], scalar1=column_factor[:, 0:1])
+            else:
+                nc.vector.scalar_tensor_tensor(
+                    out=result_of(2 * e), in0=banks[2 * e - 1][:], scalar=row_factor[:, 0:1], in1=boths[e][:],
+                    op0=ALU.mult, op1=ALU.add,
+                )
+
+        def finish_odd(e):
+            if e == COLS // 2 - 1:
+                nc.vector.tensor_scalar_mul(out=result_of(2 * e + 1), in0=boths[e][:], scalar1=column_factor[:, 0:1])
+            else:
+                nc.gpsimd.tensor_add(out=result_of(2 * e + 1), in0=boths[e][:], in1=evens[e + 1][:])
+            if (2 * e + 1) % CHUNK_COLS == CHUNK_COLS - 1:
+                store((2 * e + 1) // CHUNK_COLS)
+
+        for step in range(N_CHUNKS + LAG):
+            new, old, last = step, step - LAG, step - 1
+            ys = []
+            if new < N_CHUNKS:
+                ys = [multiply(new, fb)[:] for fb in range(KEPT)] + [y_kept[:, new * CHUNK : (new + 1) * CHUNK]]
+            if 0 <= last < N_CHUNKS:
+                sum_over_rows(last)
+            if old >= 0:
+                e = old * CHUNK_COLS // 2
+                turn_back(2 * e)
+                turn_back(2 * e + 1)
+                take_even(e)
+                add_pair(e)
+                if e > 0:
+                    finish_odd(e - 1)
+            for fb in range(TENSOR_BLOCKS, len(ys)):
+                norm_relu(new, fb, ys[fb])
+            if 0 <= last < N_CHUNKS:
+                mend_row_ends(last)
+            if old >= 0:
+                turn_back(2 * e + 2)
+                turn_back(2 * e + 3)
+                take_even(e + 1)
+                add_pair(e + 1)
+                finish_even(e)
+                finish_odd(e)
+                finish_even(e + 1)
+            if new < N_CHUNKS:
+                for fb in range(TENSOR_BLOCKS):
+                    norm_relu(new, fb, ys[fb])
+                scale_row_ends_split(new)
+                scale_row_ends_padded(new)
+        finish_odd(COLS // 2 - 1)

@@ -372,7 +372,7 @@ def tile_graphconvolutionbatch_kernel(tc, H, W, gamma, beta, out):
             ends = ends.rearrange("p g (r b) -> p g r b", b=BATCH)[:, :, 0 : ROWS : ROWS - 1, :]
             pairs = both_rows[chunk][:].rearrange("p i (q n) -> p (i q) n", q=CHUNK_COLS)
             pairs = pairs.rearrange("p g (k b) -> p g k b", b=BATCH)[:, :, 0 : ROW_PAIRS : ROW_PAIRS - 1, :]
-            nc.vector.tensor_copy(out=ends, in_=pairs)
+            nc.gpsimd.tensor_copy(out=ends, in_=pairs)
 
         def turn_back(c):
             chunk, col = c // CHUNK_COLS, c % CHUNK_COLS
@@ -444,6 +444,7 @@ def tile_graphconvolutionbatch_kernel(tc, H, W, gamma, beta, out):
                 ys = [multiply(new, fb)[:] for fb in range(KEPT)] + [y_kept[:, new * CHUNK : (new + 1) * CHUNK]]
             if 0 <= last < N_CHUNKS:
                 sum_over_rows(last)
+                mend_row_ends(last)
             if old >= 0:
                 e = old * CHUNK_COLS // 2
                 turn_back(2 * e)
@@ -454,8 +455,6 @@ def tile_graphconvolutionbatch_kernel(tc, H, W, gamma, beta, out):
                     finish_odd(e - 1)
             for fb in range(TENSOR_BLOCKS, len(ys)):
                 norm_relu(new, fb, ys[fb])
-            if 0 <= last < N_CHUNKS:
-                mend_row_ends(last)
             if old >= 0:
                 turn_back(2 * e + 2)
                 turn_back(2 * e + 3)

@@ -31,8 +31,8 @@ HALF = CHUNK // 2
 ODD_AT = HALF + 8
 SPLIT = 2 * ODD_AT
 N_PADDED = 4
-VECTOR_BLOCKS = 2
-TENSOR_BLOCKS = F_BLOCKS - VECTOR_BLOCKS
+TENSOR_BLOCKS = (2, 3)
+VECTOR_BLOCKS = tuple(F_BLOCKS - n for n in TENSOR_BLOCKS)
 KEPT = F_BLOCKS - 1
 LOAD_BUFS = 6
 AHEAD = 2
@@ -43,6 +43,14 @@ D6 = (6.0 + EPS_DEG) ** -0.5
 D4 = (4.0 + EPS_DEG) ** -0.5
 
 FLOPS = 2 * NODES * IN_DIM * OUT_DIM
+
+
+def tensor_blocks(chunk):
+    return TENSOR_BLOCKS[chunk % 2]
+
+
+def vector_blocks(chunk):
+    return VECTOR_BLOCKS[chunk % 2]
 
 
 def column_runs(chunk):
@@ -98,7 +106,10 @@ def tile_graphconvolutionbatch_kernel(tc, H, W, gamma, beta, out):
         )
         one = const.tile([P, 1], F32)
         nc.vector.memset(one[:], 1.0)
-        nc.scalar.sqrt(out=one[:], in_=one[:])
+        root = const.tile([P, 1], F32)
+        nc.scalar.sqrt(out=root[:], in_=one[:])
+        eps = const.tile([P, 1], F32)
+        nc.vector.tensor_scalar_mul(out=eps[:], in0=one[:], scalar1=EPS_BN)
 
         ident = const.tile([P, P], F32)
         make_identity(nc, ident[:])
@@ -113,6 +124,7 @@ def tile_graphconvolutionbatch_kernel(tc, H, W, gamma, beta, out):
         w_scales = const.tile([P, OUT_DIM], U8, align_bytes=64)
         gb_rows_f32 = const.tile([P, P], F32)
         gb = const.tile([P, 2, 2, F_BLOCKS], F32)
+        weighed = const.tile([P, 2, 2, F_BLOCKS], F32)
 
         def quantise_weights():
             nc.vector.tensor_copy(out=w_grouped[:], in_=w_raw[:].rearrange("p t f -> p f t"))
@@ -131,6 +143,7 @@ def tile_graphconvolutionbatch_kernel(tc, H, W, gamma, beta, out):
                     in0=bank[:, 0 : 2 * F_BLOCKS].rearrange("p (s f) -> p s f", s=2),
                     scalar1=factor,
                 )
+            nc.vector.tensor_copy(out=weighed[:, :, 0, :], in_=gb[:, :, 0, :])
 
         on_row_edge = const.tile([P, 1], F32)
         nc.vector.tensor_reduce(
@@ -153,15 +166,14 @@ def tile_graphconvolutionbatch_kernel(tc, H, W, gamma, beta, out):
             op1=ALU.add,
         )
 
-        n_runs = TENSOR_BLOCKS * CHUNK_COLS
         padded = []
         split = []
         for i in range(N_PADDED):
-            pad_tile = const.tile([P, (n_runs + 1) * PITCH], F32, name="padded%d" % i)
+            pad_tile = const.tile([P, (max(TENSOR_BLOCKS) * CHUNK_COLS + 1) * PITCH], F32, name="padded%d" % i)
             nc.gpsimd.memset(pad_tile[:].rearrange("p (g s) -> p g s", s=PITCH)[:, :, 0:RUN_AT], 0.0)
             padded.append(pad_tile)
-            split_tile = const.tile([P, VECTOR_BLOCKS * SPLIT + P], F32, name="split%d" % i)
-            gaps = split_tile[:, 0 : VECTOR_BLOCKS * SPLIT].rearrange("p (g w) -> p g w", w=ODD_AT)[:, :, HALF:ODD_AT]
+            split_tile = const.tile([P, max(VECTOR_BLOCKS) * SPLIT + P], F32, name="split%d" % i)
+            gaps = split_tile[:, 0 : max(VECTOR_BLOCKS) * SPLIT].rearrange("p (g w) -> p g w", w=ODD_AT)[:, :, HALF:ODD_AT]
             nc.gpsimd.memset(gaps, 0.0)
             split.append(split_tile)
 
@@ -169,7 +181,8 @@ def tile_graphconvolutionbatch_kernel(tc, H, W, gamma, beta, out):
         h_scales = const.tile([P, NODES], U8, align_bytes=64)
         stats = const.tile([P, KEPT, N_CHUNKS, 6], F32)
         y_kept = const.tile([P, NODES], F32)
-        kept_sums = const.tile([P, 2, N_CHUNKS], F32)
+        kept_sums = const.tile([P, N_CHUNKS, 2], F32)
+        kept_totals = const.tile([P, 2], F32)
         minus_first = const.tile([P, 1], F32)
         squares = const.tile([P, CHUNK], F32)
 
@@ -214,7 +227,7 @@ def tile_graphconvolutionbatch_kernel(tc, H, W, gamma, beta, out):
         def keep(chunk, y):
             nodes = slice(chunk * CHUNK, (chunk + 1) * CHUNK)
             nc.scalar.activation(
-                out=y_kept[:, nodes], in_=y[:], func=ACT.Identity, accum_out=kept_sums[:, 0, chunk : chunk + 1]
+                out=y_kept[:, nodes], in_=y[:], func=ACT.Identity, accum_out=kept_sums[:, chunk, 0:1]
             )
             if chunk == 0:
                 nc.scalar.mul(out=minus_first[:], in_=kept_sums[:, 0, 0:1], mul=-1.0 / CHUNK)
@@ -226,8 +239,12 @@ def tile_graphconvolutionbatch_kernel(tc, H, W, gamma, beta, out):
                 in_=y_kept[:, nodes],
                 func=ACT.Square,
                 bias=minus_first[:, 0:1],
-                accum_out=kept_sums[:, 1, chunk : chunk + 1],
+                accum_out=kept_sums[:, chunk, 1:2],
             )
+            if chunk == 0:
+                nc.gpsimd.tensor_copy(out=kept_totals[:], in_=kept_sums[:, 0, :])
+            else:
+                nc.gpsimd.tensor_add(out=kept_totals[:], in0=kept_totals[:], in1=kept_sums[:, chunk, :])
 
         groups = {}
         for chunk in range(AHEAD):
@@ -255,38 +272,34 @@ def tile_graphconvolutionbatch_kernel(tc, H, W, gamma, beta, out):
         square(N_CHUNKS - 1)
 
         mean_var = const.tile([P, F_BLOCKS, 2], F32)
-        kept_totals = const.tile([P, 2], F32)
-        off_first = const.tile([P, 2], F32)
-
-        def aggregate(fb):
-            nc.vector.bn_aggr(out=mean_var[:, fb, :], in_=stats[:, fb, :, :].rearrange("p j s -> p (j s)"))
-
-        aggregate(0)
-        nc.vector.tensor_reduce(out=kept_totals[:], in_=kept_sums[:], axis=AXIS.X, op=ALU.add)
-        aggregate(1)
-        nc.vector.tensor_scalar_mul(out=mean_var[:, KEPT, :], in0=kept_totals[:], scalar1=1.0 / NODES)
-        nc.vector.tensor_scalar(
-            out=off_first[:, 0:1], in0=kept_totals[:, 0:1], scalar1=1.0 / NODES, scalar2=minus_first[:, 0:1],
-            op0=ALU.mult, op1=ALU.add,
-        )
-        aggregate(2)
-        nc.vector.tensor_mul(out=off_first[:, 1:2], in0=off_first[:, 0:1], in1=off_first[:, 0:1])
-        nc.vector.tensor_sub(out=mean_var[:, KEPT, 1:2], in0=mean_var[:, KEPT, 1:2], in1=off_first[:, 1:2])
         std = const.tile([P, F_BLOCKS], F32)
-        nc.vector.tensor_scalar_add(out=std[:], in0=mean_var[:, :, 1], scalar1=EPS_BN)
-        nc.scalar.sqrt(out=std[:], in_=std[:])
+        square_off = const.tile([P, 1], F32)
+        eps_off = const.tile([P, 1], F32)
+        nc.scalar.activation(
+            out=square_off[:], in_=kept_totals[:, 0:1], func=ACT.Square, bias=minus_first[:, 0:1], scale=1.0 / NODES
+        )
+        nc.scalar.mul(out=mean_var[:, KEPT, 0:1], in_=kept_totals[:, 0:1], mul=1.0 / NODES)
+        nc.scalar.activation(out=eps_off[:], in_=square_off[:], func=ACT.Identity, bias=eps[:, 0:1], scale=-1.0)
+        nc.scalar.activation(
+            out=std[:, KEPT:F_BLOCKS], in_=kept_totals[:, 1:2], func=ACT.Sqrt, bias=eps_off[:, 0:1], scale=1.0 / NODES
+        )
+        for fb in range(KEPT):
+            nc.vector.bn_aggr(out=mean_var[:, fb, :], in_=stats[:, fb, :, :].rearrange("p j s -> p (j s)"))
+        nc.scalar.activation(out=std[:, 0:KEPT], in_=mean_var[:, 0:KEPT, 1], func=ACT.Sqrt, bias=eps[:, 0:1])
+        nc.vector.tensor_mul(
+            out=weighed[:, :, 1, :],
+            in0=gb[:, :, 0, :],
+            in1=mean_var[:, :, 0].unsqueeze(1).to_broadcast([P, 2, F_BLOCKS]),
+        )
         rstd = const.tile([P, F_BLOCKS], F32)
         nc.vector.reciprocal(out=rstd[:], in_=std[:])
         coeffs = const.tile([P, 2, 2, F_BLOCKS], F32)
-        mean_gain = const.tile([P, 2, F_BLOCKS], F32)
-        wide = [P, 2, F_BLOCKS]
         nc.vector.tensor_mul(
-            out=coeffs[:, :, 0, :], in0=gb[:, :, 0, :], in1=rstd[:].unsqueeze(1).to_broadcast(wide)
+            out=coeffs[:].rearrange("p i s f -> p (i s) f"),
+            in0=weighed[:].rearrange("p i s f -> p (i s) f"),
+            in1=rstd[:].unsqueeze(1).to_broadcast([P, 4, F_BLOCKS]),
         )
-        nc.vector.tensor_mul(
-            out=mean_gain[:], in0=coeffs[:, :, 0, :], in1=mean_var[:, :, 0].unsqueeze(1).to_broadcast(wide)
-        )
-        nc.vector.tensor_sub(out=coeffs[:, :, 1, :], in0=gb[:, :, 1, :], in1=mean_gain[:])
+        nc.vector.tensor_sub(out=coeffs[:, :, 1, :], in0=gb[:, :, 1, :], in1=coeffs[:, :, 1, :])
 
         row_sums = {}
         evens = {}
@@ -297,13 +310,13 @@ def tile_graphconvolutionbatch_kernel(tc, H, W, gamma, beta, out):
         def norm_relu(chunk, fb, y):
             for first, count, on_edge in column_runs(chunk):
                 coeff = coeffs[:, 1 if on_edge else 0, :, :]
-                if fb < TENSOR_BLOCKS:
+                if fb < tensor_blocks(chunk):
                     at = fb * CHUNK_COLS + first
                     runs = padded[chunk % N_PADDED][:].rearrange("p (g s) -> p g s", s=PITCH)
                     z_out = runs[:, at : at + count, RUN_AT:PITCH]
                     y_in = y.rearrange("p (q n) -> p q n", n=P)[:, first : first + count, :]
                 else:
-                    at = (fb - TENSOR_BLOCKS) * SPLIT
+                    at = (fb - tensor_blocks(chunk)) * SPLIT
                     by_parity = split[chunk % N_PADDED][:, at : at + SPLIT].rearrange("p (t m b) -> p t m b", t=2, b=BATCH)
                     pairs = slice(first * ROW_PAIRS, (first + count) * ROW_PAIRS)
                     z_out = by_parity[:, :, pairs, :]
@@ -318,7 +331,7 @@ def tile_graphconvolutionbatch_kernel(tc, H, W, gamma, beta, out):
 
         def scale_row_ends_padded(chunk):
             runs = padded[chunk % N_PADDED][:].rearrange("p (g s) -> p g s", s=PITCH)
-            n_runs = TENSOR_BLOCKS * CHUNK_COLS
+            n_runs = tensor_blocks(chunk) * CHUNK_COLS
 
             def scale(some, factor):
                 ends = some[:, :, RUN_AT:PITCH].rearrange("p g (r b) -> p g r b", b=BATCH)[:, :, 0 : ROWS : ROWS - 1, :]
@@ -331,7 +344,7 @@ def tile_graphconvolutionbatch_kernel(tc, H, W, gamma, beta, out):
 
         def scale_row_ends_split(chunk):
             apart = ODD_AT + P // 2 - BATCH
-            for i in range(VECTOR_BLOCKS):
+            for i in range(vector_blocks(chunk)):
                 ends = (
                     split[chunk % N_PADDED][:, i * SPLIT : i * SPLIT + 2 * apart]
                     .rearrange("p (t w) -> p t w", t=2)[:, :, 0:HALF]
@@ -345,14 +358,14 @@ def tile_graphconvolutionbatch_kernel(tc, H, W, gamma, beta, out):
 
         def sum_over_rows(chunk):
             z = split[chunk % N_PADDED]
-            both = halves.tile([P, VECTOR_BLOCKS, HALF], F32, name="both_rows")
-            total = sums.tile([P, VECTOR_BLOCKS, CHUNK], F32, name="total")
-            for i in range(VECTOR_BLOCKS):
+            both = halves.tile([P, vector_blocks(chunk), HALF], F32, name="both_rows")
+            total = sums.tile([P, vector_blocks(chunk), CHUNK], F32, name="total")
+            for i in range(vector_blocks(chunk)):
                 at = i * SPLIT
                 nc.vector.tensor_add(
                     out=both[:, i, :], in0=z[:, at : at + HALF], in1=z[:, at + ODD_AT : at + ODD_AT + HALF]
                 )
-            for i in range(VECTOR_BLOCKS):
+            for i in range(vector_blocks(chunk)):
                 at = i * SPLIT + BATCH
                 outer = (
                     z[:, at : at + 2 * (ODD_AT - 2 * BATCH)]
@@ -378,12 +391,12 @@ def tile_graphconvolutionbatch_kernel(tc, H, W, gamma, beta, out):
             chunk, col = c // CHUNK_COLS, c % CHUNK_COLS
             pad_tile = padded[chunk % N_PADDED]
             parts = []
-            for fb in range(TENSOR_BLOCKS):
+            for fb in range(tensor_blocks(chunk)):
                 at = (fb * CHUNK_COLS + col) * PITCH + RUN_AT
                 for shift in (-BATCH, 0, BATCH):
                     parts.append((fb, pad_tile[:, at + shift : at + shift + P]))
-            for i in range(VECTOR_BLOCKS):
-                parts.append((TENSOR_BLOCKS + i, row_sums[chunk][:, i, col * P : (col + 1) * P]))
+            for i in range(vector_blocks(chunk)):
+                parts.append((tensor_blocks(chunk) + i, row_sums[chunk][:, i, col * P : (col + 1) * P]))
             bank = psum_t.tile([P, OUT_DIM], F32, tag="t", name="bank")
             for i, (fb, source) in enumerate(parts):
                 nc.tensor.matmul(
@@ -402,11 +415,11 @@ def tile_graphconvolutionbatch_kernel(tc, H, W, gamma, beta, out):
                 results[group] = stores.tile([P, CHUNK_COLS, OUT_DIM], F32, name="result")
             return results[group][:, c % CHUNK_COLS, :]
 
-        def store(group):
+        def store(group, first, last):
             for b in range(BATCH):
                 nc.sync.dma_start(
-                    out=out_view[b, :, group * CHUNK_COLS : (group + 1) * CHUNK_COLS, :],
-                    in_=results[group][b : P : BATCH, :, :],
+                    out=out_view[b, :, group * CHUNK_COLS + first : group * CHUNK_COLS + last, :],
+                    in_=results[group][b : P : BATCH, first:last, :],
                 )
 
         def take_even(e):
@@ -434,8 +447,11 @@ def tile_graphconvolutionbatch_kernel(tc, H, W, gamma, beta, out):
                 nc.vector.tensor_scalar_mul(out=result_of(2 * e + 1), in0=boths[e][:], scalar1=column_factor[:, 0:1])
             else:
                 nc.gpsimd.tensor_add(out=result_of(2 * e + 1), in0=boths[e][:], in1=evens[e + 1][:])
-            if (2 * e + 1) % CHUNK_COLS == CHUNK_COLS - 1:
-                store((2 * e + 1) // CHUNK_COLS)
+            group, last = (2 * e + 1) // CHUNK_COLS, (2 * e + 1) % CHUNK_COLS + 1
+            if group == N_CHUNKS - 1:
+                store(group, last - 2, last)
+            elif last == CHUNK_COLS:
+                store(group, 0, CHUNK_COLS)
 
         for step in range(N_CHUNKS + LAG):
             new, old, last = step, step - LAG, step - 1
@@ -453,8 +469,11 @@ def tile_graphconvolutionbatch_kernel(tc, H, W, gamma, beta, out):
                 add_pair(e)
                 if e > 0:
                     finish_odd(e - 1)
-            for fb in range(TENSOR_BLOCKS, len(ys)):
-                norm_relu(new, fb, ys[fb])
+            if new < N_CHUNKS:
+                for fb in range(tensor_blocks(new), F_BLOCKS):
+                    norm_relu(new, fb, ys[fb])
+                if new == 0:
+                    scale_row_ends_split(new)
             if old >= 0:
                 turn_back(2 * e + 2)
                 turn_back(2 * e + 3)
@@ -464,8 +483,9 @@ def tile_graphconvolutionbatch_kernel(tc, H, W, gamma, beta, out):
                 finish_odd(e)
                 finish_even(e + 1)
             if new < N_CHUNKS:
-                for fb in range(TENSOR_BLOCKS):
+                for fb in range(tensor_blocks(new)):
                     norm_relu(new, fb, ys[fb])
-                scale_row_ends_split(new)
+                if new > 0:
+                    scale_row_ends_split(new)
                 scale_row_ends_padded(new)
         finish_odd(COLS // 2 - 1)

@@ -28,12 +28,12 @@ ROW_PAIRS = ROWS // 2
 PITCH = P + 4
 RUN_AT = 4
 HALF = CHUNK // 2
-ODD_AT = HALF + 8
-SPLIT = 2 * ODD_AT
 N_PADDED = 4
-TENSOR_BLOCKS = (2, 3)
-VECTOR_BLOCKS = tuple(F_BLOCKS - n for n in TENSOR_BLOCKS)
 KEPT = F_BLOCKS - 1
+PSUM_ORDER = (2, 0, 1)
+VECTOR_BLOCKS = 2
+ODD_AT = VECTOR_BLOCKS * HALF + 8
+SPLIT = 2 * ODD_AT + HALF + 8
 LOAD_BUFS = 6
 AHEAD = 2
 LAG = 2
@@ -45,12 +45,12 @@ D4 = (4.0 + EPS_DEG) ** -0.5
 FLOPS = 2 * NODES * IN_DIM * OUT_DIM
 
 
-def tensor_blocks(chunk):
-    return TENSOR_BLOCKS[chunk % 2]
-
-
 def vector_blocks(chunk):
-    return VECTOR_BLOCKS[chunk % 2]
+    return 0 if chunk in (0, N_CHUNKS - 1) else VECTOR_BLOCKS
+
+
+def tensor_blocks(chunk):
+    return F_BLOCKS - vector_blocks(chunk)
 
 
 def column_runs(chunk):
@@ -169,12 +169,11 @@ def tile_graphconvolutionbatch_kernel(tc, H, W, gamma, beta, out):
         padded = []
         split = []
         for i in range(N_PADDED):
-            pad_tile = const.tile([P, (max(TENSOR_BLOCKS) * CHUNK_COLS + 1) * PITCH], F32, name="padded%d" % i)
+            pad_tile = const.tile([P, (F_BLOCKS * CHUNK_COLS + 1) * PITCH], F32, name="padded%d" % i)
             nc.gpsimd.memset(pad_tile[:].rearrange("p (g s) -> p g s", s=PITCH)[:, :, 0:RUN_AT], 0.0)
             padded.append(pad_tile)
-            split_tile = const.tile([P, max(VECTOR_BLOCKS) * SPLIT + P], F32, name="split%d" % i)
-            gaps = split_tile[:, 0 : max(VECTOR_BLOCKS) * SPLIT].rearrange("p (g w) -> p g w", w=ODD_AT)[:, :, HALF:ODD_AT]
-            nc.gpsimd.memset(gaps, 0.0)
+            split_tile = const.tile([P, SPLIT], F32, name="split%d" % i)
+            nc.gpsimd.memset(split_tile[:], 0.0)
             split.append(split_tile)
 
         h_codes = const.tile([P, NODES], U32, align_bytes=64)
@@ -316,10 +315,10 @@ def tile_graphconvolutionbatch_kernel(tc, H, W, gamma, beta, out):
                     z_out = runs[:, at : at + count, RUN_AT:PITCH]
                     y_in = y.rearrange("p (q n) -> p q n", n=P)[:, first : first + count, :]
                 else:
-                    at = (fb - tensor_blocks(chunk)) * SPLIT
-                    by_parity = split[chunk % N_PADDED][:, at : at + SPLIT].rearrange("p (t m b) -> p t m b", t=2, b=BATCH)
+                    by_parity = split[chunk % N_PADDED][:, 0 : 2 * ODD_AT].rearrange("p (t w) -> p t w", t=2)
+                    at = (fb - tensor_blocks(chunk)) * HALF + first * ROWS
+                    z_out = by_parity[:, :, at : at + count * ROWS].rearrange("p t (m b) -> p t m b", b=BATCH)
                     pairs = slice(first * ROW_PAIRS, (first + count) * ROW_PAIRS)
-                    z_out = by_parity[:, :, pairs, :]
                     y_in = y.rearrange("p (m t b) -> p t m b", t=2, b=BATCH)[:, :, pairs, :]
                 nc.scalar.activation(
                     out=z_out,
@@ -329,44 +328,40 @@ def tile_graphconvolutionbatch_kernel(tc, H, W, gamma, beta, out):
                     scale=coeff[:, 0, fb : fb + 1],
                 )
 
-        def scale_row_ends_padded(chunk):
-            runs = padded[chunk % N_PADDED][:].rearrange("p (g s) -> p g s", s=PITCH)
+        def factors(chunk):
+            edge = [(first, CHUNK_COLS, (D4 / D6) / (D6 / D9)) for first, count, on_edge in column_runs(chunk) if on_edge]
+            return [(0, 1, D6 / D9)] + edge
+
+        def scale_split(chunk):
+            n_runs = vector_blocks(chunk) * CHUNK_COLS
+            apart = ODD_AT + ROWS - BATCH
+            ends = split[chunk % N_PADDED][:, 0 : 2 * apart].rearrange("p (t w) -> p t w", t=2)
+            ends = ends[:, :, 0 : n_runs * ROWS].rearrange("p t (g n) -> p t g n", n=ROWS)[:, :, :, 0:BATCH]
+            for first, step, factor in factors(chunk):
+                some = ends[:, :, first:n_runs:step, :]
+                nc.scalar.mul(out=some, in_=some, mul=factor)
+
+        def scale_padded(chunk):
             n_runs = tensor_blocks(chunk) * CHUNK_COLS
-
-            def scale(some, factor):
-                ends = some[:, :, RUN_AT:PITCH].rearrange("p g (r b) -> p g r b", b=BATCH)[:, :, 0 : ROWS : ROWS - 1, :]
-                nc.scalar.mul(out=ends, in_=ends, mul=factor)
-
-            scale(runs[:, 0:n_runs, :], D6 / D9)
-            for first, count, on_edge in column_runs(chunk):
-                if on_edge:
-                    scale(runs[:, first : n_runs : CHUNK_COLS, :], (D4 / D6) / (D6 / D9))
-
-        def scale_row_ends_split(chunk):
-            apart = ODD_AT + P // 2 - BATCH
-            for i in range(vector_blocks(chunk)):
-                ends = (
-                    split[chunk % N_PADDED][:, i * SPLIT : i * SPLIT + 2 * apart]
-                    .rearrange("p (t w) -> p t w", t=2)[:, :, 0:HALF]
-                    .rearrange("p t (q n) -> p t q n", q=CHUNK_COLS)[:, :, :, 0:BATCH]
-                )
-                for first, count, on_edge in column_runs(chunk):
-                    some = ends[:, :, first : first + count, :]
-                    nc.scalar.mul(out=some, in_=some, mul=D4 / D6 if on_edge else D6 / D9)
+            runs = padded[chunk % N_PADDED][:].rearrange("p (g s) -> p g s", s=PITCH)
+            ends = runs[:, 0:n_runs, RUN_AT:PITCH].rearrange("p g (r b) -> p g r b", b=BATCH)
+            for first, step, factor in factors(chunk):
+                some = ends[:, first:n_runs:step, 0 : ROWS : ROWS - 1, :]
+                nc.gpsimd.tensor_scalar(out=some, in0=some, scalar1=factor, scalar2=0.0, op0=ALU.mult, op1=ALU.add)
 
         both_rows = {}
 
         def sum_over_rows(chunk):
             z = split[chunk % N_PADDED]
-            both = halves.tile([P, vector_blocks(chunk), HALF], F32, name="both_rows")
-            total = sums.tile([P, vector_blocks(chunk), CHUNK], F32, name="total")
+            both = halves.tile([P, VECTOR_BLOCKS, HALF], F32, name="both_rows")
+            total = sums.tile([P, VECTOR_BLOCKS, CHUNK], F32, name="total")
             for i in range(vector_blocks(chunk)):
-                at = i * SPLIT
+                at = i * HALF
                 nc.vector.tensor_add(
                     out=both[:, i, :], in0=z[:, at : at + HALF], in1=z[:, at + ODD_AT : at + ODD_AT + HALF]
                 )
             for i in range(vector_blocks(chunk)):
-                at = i * SPLIT + BATCH
+                at = i * HALF + BATCH
                 outer = (
                     z[:, at : at + 2 * (ODD_AT - 2 * BATCH)]
                     .rearrange("p (t w) -> p t w", t=2)[:, ::-1, 0:HALF]
@@ -453,39 +448,47 @@ def tile_graphconvolutionbatch_kernel(tc, H, W, gamma, beta, out):
             elif last == CHUNK_COLS:
                 store(group, 0, CHUNK_COLS)
 
+        products = {}
+
+        def multiply_again(chunk):
+            if chunk < N_CHUNKS:
+                products[chunk] = {fb: multiply(chunk, fb)[:] for fb in PSUM_ORDER}
+                products[chunk][KEPT] = y_kept[:, chunk * CHUNK : (chunk + 1) * CHUNK]
+
+        multiply_again(0)
         for step in range(N_CHUNKS + LAG):
-            new, old, last = step, step - LAG, step - 1
-            ys = []
-            if new < N_CHUNKS:
-                ys = [multiply(new, fb)[:] for fb in range(KEPT)] + [y_kept[:, new * CHUNK : (new + 1) * CHUNK]]
+            new, last = step, step - 1
+            old = {1: 0, 2: -1}.get(step, step - LAG)
             if 0 <= last < N_CHUNKS:
-                sum_over_rows(last)
-                mend_row_ends(last)
+                if vector_blocks(last) > 0:
+                    sum_over_rows(last)
+                    mend_row_ends(last)
+                scale_padded(last)
             if old >= 0:
                 e = old * CHUNK_COLS // 2
                 turn_back(2 * e)
                 turn_back(2 * e + 1)
+            if new < N_CHUNKS:
+                norm_relu(new, 2, products[new][2])
+                norm_relu(new, 3, products[new][3])
+            if old >= 0:
                 take_even(e)
                 add_pair(e)
                 if e > 0:
                     finish_odd(e - 1)
-            if new < N_CHUNKS:
-                for fb in range(tensor_blocks(new), F_BLOCKS):
-                    norm_relu(new, fb, ys[fb])
-                if new == 0:
-                    scale_row_ends_split(new)
-            if old >= 0:
                 turn_back(2 * e + 2)
                 turn_back(2 * e + 3)
+            if new < N_CHUNKS:
+                if vector_blocks(new) > 0:
+                    scale_split(new)
+                norm_relu(new, 0, products[new][0])
+            if old >= 0:
                 take_even(e + 1)
                 add_pair(e + 1)
                 finish_even(e)
                 finish_odd(e)
                 finish_even(e + 1)
             if new < N_CHUNKS:
-                for fb in range(tensor_blocks(new)):
-                    norm_relu(new, fb, ys[fb])
-                if new > 0:
-                    scale_row_ends_split(new)
-                scale_row_ends_padded(new)
+                norm_relu(new, 1, products[new][1])
+            multiply_again(new + 1)
         finish_odd(COLS // 2 - 1)

@@ -347,7 +347,7 @@ def tile_graphconvolutionbatch_kernel(tc, H, W, gamma, beta, out):
             ends = runs[:, 0:n_runs, RUN_AT:PITCH].rearrange("p g (r b) -> p g r b", b=BATCH)
             for first, step, factor in factors(chunk):
                 some = ends[:, first:n_runs:step, 0 : ROWS : ROWS - 1, :]
-                nc.gpsimd.tensor_scalar(out=some, in0=some, scalar1=factor, scalar2=0.0, op0=ALU.mult, op1=ALU.add)
+                nc.scalar.mul(out=some, in_=some, mul=factor)
 
         both_rows = {}
 
@@ -463,13 +463,15 @@ def tile_graphconvolutionbatch_kernel(tc, H, W, gamma, beta, out):
                 if vector_blocks(last) > 0:
                     sum_over_rows(last)
                     mend_row_ends(last)
-                scale_padded(last)
             if old >= 0:
                 e = old * CHUNK_COLS // 2
                 turn_back(2 * e)
                 turn_back(2 * e + 1)
             if new < N_CHUNKS:
                 norm_relu(new, 2, products[new][2])
+            if 0 < last < N_CHUNKS:
+                scale_padded(last)
+            if new < N_CHUNKS:
                 norm_relu(new, 3, products[new][3])
             if old >= 0:
                 take_even(e)
@@ -490,5 +492,7 @@ def tile_graphconvolutionbatch_kernel(tc, H, W, gamma, beta, out):
                 finish_even(e + 1)
             if new < N_CHUNKS:
                 norm_relu(new, 1, products[new][1])
+                if new == 0:
+                    scale_padded(0)
             multiply_again(new + 1)
         finish_odd(COLS // 2 - 1)

@@ -70,12 +70,11 @@ def tile_graphconvolutionbatch_kernel(tc, H, W, gamma, beta, out):
         const = ctx.enter_context(tc.tile_pool(name="const", bufs=1))
         loads = ctx.enter_context(tc.tile_pool(name="loads", bufs=LOAD_BUFS))
         stage = ctx.enter_context(tc.tile_pool(name="stage", bufs=3))
-        sums = ctx.enter_context(tc.tile_pool(name="sums", bufs=3))
+        sums = ctx.enter_context(tc.tile_pool(name="sums", bufs=4))
         halves = ctx.enter_context(tc.tile_pool(name="halves", bufs=2))
         columns = ctx.enter_context(tc.tile_pool(name="columns", bufs=4))
         stores = ctx.enter_context(tc.tile_pool(name="stores", bufs=3))
-        psum_y = ctx.enter_context(tc.psum_pool(name="psum_y", bufs=4))
-        psum_t = ctx.enter_context(tc.psum_pool(name="psum_t", bufs=4))
+        psum = ctx.enter_context(tc.psum_pool(name="psum", bufs=8))
 
         h_raw = {}
 
@@ -135,7 +134,7 @@ def tile_graphconvolutionbatch_kernel(tc, H, W, gamma, beta, out):
             )
 
         def turn_gamma_beta():
-            bank = psum_t.tile([P, P], F32, tag="t", name="gb_bank")
+            bank = psum.tile([P, P], F32, tag="bank", name="gb_bank")
             nc.tensor.transpose(bank[:], gb_rows_f32[:], ident[:])
             for i, factor in enumerate((D9 * D9, D6 * D9)):
                 nc.vector.tensor_scalar_mul(
@@ -188,7 +187,7 @@ def tile_graphconvolutionbatch_kernel(tc, H, W, gamma, beta, out):
         def multiply(chunk, fb):
             nodes = slice(chunk * CHUNK, (chunk + 1) * CHUNK)
             feats = slice(fb * P, (fb + 1) * P)
-            y = psum_y.tile([P, CHUNK], F32, tag="y")
+            y = psum.tile([P, CHUNK], F32, tag="bank")
             nc.tensor.matmul_mx(
                 out=y[:],
                 lhsT=w_codes[:, feats].bitcast(FP8X4),
@@ -204,7 +203,7 @@ def tile_graphconvolutionbatch_kernel(tc, H, W, gamma, beta, out):
             grouped = stage.tile([P, CHUNK * PACK], BF16, align_bytes=64, name="grouped")
             grouped_words = grouped[:].bitcast(F32).rearrange("p (n u) -> p n u", u=2)
             for half in range(2):
-                turned = psum_t.tile([P, 2, 2 * P], F32, tag="t", name="turned")
+                turned = psum.tile([P, 2, 2 * P], F32, tag="bank", name="turned")
                 for i in range(2):
                     words = h_raw[chunk][:, 2 * half + i, :].bitcast(F32)
                     for u in range(2):
@@ -392,7 +391,7 @@ def tile_graphconvolutionbatch_kernel(tc, H, W, gamma, beta, out):
                     parts.append((fb, pad_tile[:, at + shift : at + shift + P]))
             for i in range(vector_blocks(chunk)):
                 parts.append((tensor_blocks(chunk) + i, row_sums[chunk][:, i, col * P : (col + 1) * P]))
-            bank = psum_t.tile([P, OUT_DIM], F32, tag="t", name="bank")
+            bank = psum.tile([P, OUT_DIM], F32, tag="bank", name="bank")
             for i, (fb, source) in enumerate(parts):
                 nc.tensor.matmul(
                     out=bank[:, fb * P : (fb + 1) * P],
@@ -450,49 +449,58 @@ def tile_graphconvolutionbatch_kernel(tc, H, W, gamma, beta, out):
 
         products = {}
 
-        def multiply_again(chunk):
+        def multiply_again(chunk, some):
             if chunk < N_CHUNKS:
-                products[chunk] = {fb: multiply(chunk, fb)[:] for fb in PSUM_ORDER}
-                products[chunk][KEPT] = y_kept[:, chunk * CHUNK : (chunk + 1) * CHUNK]
+                for fb in some:
+                    products[chunk, fb] = multiply(chunk, fb)[:]
+                products[chunk, KEPT] = y_kept[:, chunk * CHUNK : (chunk + 1) * CHUNK]
 
-        multiply_again(0)
+        def sum_rows(chunk):
+            sum_over_rows(chunk)
+            mend_row_ends(chunk)
+
+        multiply_again(0, PSUM_ORDER)
         for step in range(N_CHUNKS + LAG):
             new, last = step, step - 1
             old = {1: 0, 2: -1}.get(step, step - LAG)
-            if 0 <= last < N_CHUNKS:
-                if vector_blocks(last) > 0:
-                    sum_over_rows(last)
-                    mend_row_ends(last)
+            on_vector = new < N_CHUNKS and vector_blocks(new) > 0
             if old >= 0:
                 e = old * CHUNK_COLS // 2
                 turn_back(2 * e)
                 turn_back(2 * e + 1)
             if new < N_CHUNKS:
-                norm_relu(new, 2, products[new][2])
+                norm_relu(new, 2, products[new, 2])
             if 0 < last < N_CHUNKS:
                 scale_padded(last)
             if new < N_CHUNKS:
-                norm_relu(new, 3, products[new][3])
+                norm_relu(new, 3, products[new, 3])
+            if step == 1:
+                scale_split(new)
+                sum_rows(new)
             if old >= 0:
                 take_even(e)
                 add_pair(e)
                 if e > 0:
                     finish_odd(e - 1)
+            multiply_again(new + 1, PSUM_ORDER[:2])
+            if old >= 0:
                 turn_back(2 * e + 2)
                 turn_back(2 * e + 3)
+            if on_vector and step > 1:
+                scale_split(new)
             if new < N_CHUNKS:
-                if vector_blocks(new) > 0:
-                    scale_split(new)
-                norm_relu(new, 0, products[new][0])
+                norm_relu(new, 0, products[new, 0])
             if old >= 0:
                 take_even(e + 1)
                 add_pair(e + 1)
                 finish_even(e)
                 finish_odd(e)
                 finish_even(e + 1)
+            if on_vector and step > 1:
+                sum_rows(new)
             if new < N_CHUNKS:
-                norm_relu(new, 1, products[new][1])
+                norm_relu(new, 1, products[new, 1])
                 if new == 0:
                     scale_padded(0)
-            multiply_again(new + 1)
+            multiply_again(new + 1, PSUM_ORDER[2:])
         finish_odd(COLS // 2 - 1)

@@ -31,6 +31,7 @@ HALF = CHUNK // 2
 N_PADDED = 4
 KEPT = F_BLOCKS - 1
 PSUM_ORDER = (2, 0, 1)
+IDLE_PASSES = 20
 VECTOR_BLOCKS = 2
 ODD_AT = VECTOR_BLOCKS * HALF + 8
 SPLIT = 2 * ODD_AT + HALF + 8
@@ -46,7 +47,7 @@ FLOPS = 2 * NODES * IN_DIM * OUT_DIM
 
 
 def vector_blocks(chunk):
-    return 0 if chunk in (0, N_CHUNKS - 1) else VECTOR_BLOCKS
+    return 0 if chunk in (0, N_CHUNKS - 1) else VECTOR_BLOCKS - (chunk % 3 == 2)
 
 
 def tensor_blocks(chunk):
@@ -122,8 +123,8 @@ def tile_graphconvolutionbatch_kernel(tc, H, W, gamma, beta, out):
         w_codes = const.tile([P, OUT_DIM], U32, align_bytes=64)
         w_scales = const.tile([P, OUT_DIM], U8, align_bytes=64)
         gb_rows_f32 = const.tile([P, P], F32)
-        gb = const.tile([P, 2, 2, F_BLOCKS], F32)
-        weighed = const.tile([P, 2, 2, F_BLOCKS], F32)
+        gb = const.tile([P, 2, F_BLOCKS], F32)
+        weighed = const.tile([P, 2, F_BLOCKS], F32)
 
         def quantise_weights():
             nc.vector.tensor_copy(out=w_grouped[:], in_=w_raw[:].rearrange("p t f -> p f t"))
@@ -136,13 +137,10 @@ def tile_graphconvolutionbatch_kernel(tc, H, W, gamma, beta, out):
         def turn_gamma_beta():
             bank = psum.tile([P, P], F32, tag="bank", name="gb_bank")
             nc.tensor.transpose(bank[:], gb_rows_f32[:], ident[:])
-            for i, factor in enumerate((D9 * D9, D6 * D9)):
-                nc.vector.tensor_scalar_mul(
-                    out=gb[:, i, :, :],
-                    in0=bank[:, 0 : 2 * F_BLOCKS].rearrange("p (s f) -> p s f", s=2),
-                    scalar1=factor,
-                )
-            nc.vector.tensor_copy(out=weighed[:, :, 0, :], in_=gb[:, :, 0, :])
+            nc.vector.tensor_scalar_mul(
+                out=gb[:], in0=bank[:, 0 : 2 * F_BLOCKS].rearrange("p (s f) -> p s f", s=2), scalar1=D9 * D9
+            )
+            nc.vector.tensor_copy(out=weighed[:, 0, :], in_=gb[:, 0, :])
 
         on_row_edge = const.tile([P, 1], F32)
         nc.vector.tensor_reduce(
@@ -165,6 +163,9 @@ def tile_graphconvolutionbatch_kernel(tc, H, W, gamma, beta, out):
             op1=ALU.add,
         )
 
+        edge_source = const.tile([P, 1], F32)
+        nc.vector.tensor_scalar_mul(out=edge_source[:], in0=row_factor[:], scalar1=D6 / D9)
+
         padded = []
         split = []
         for i in range(N_PADDED):
@@ -172,7 +173,9 @@ def tile_graphconvolutionbatch_kernel(tc, H, W, gamma, beta, out):
             nc.gpsimd.memset(pad_tile[:].rearrange("p (g s) -> p g s", s=PITCH)[:, :, 0:RUN_AT], 0.0)
             padded.append(pad_tile)
             split_tile = const.tile([P, SPLIT], F32, name="split%d" % i)
-            nc.gpsimd.memset(split_tile[:], 0.0)
+            for block in range(VECTOR_BLOCKS):
+                nc.gpsimd.memset(split_tile[:, (block + 1) * HALF : (block + 1) * HALF + BATCH], 0.0)
+            nc.gpsimd.memset(split_tile[:, ODD_AT - BATCH : ODD_AT], 0.0)
             split.append(split_tile)
 
         h_codes = const.tile([P, NODES], U32, align_bytes=64)
@@ -184,10 +187,10 @@ def tile_graphconvolutionbatch_kernel(tc, H, W, gamma, beta, out):
         minus_first = const.tile([P, 1], F32)
         squares = const.tile([P, CHUNK], F32)
 
-        def multiply(chunk, fb):
+        def multiply(chunk, fb, into=None):
             nodes = slice(chunk * CHUNK, (chunk + 1) * CHUNK)
             feats = slice(fb * P, (fb + 1) * P)
-            y = psum.tile([P, CHUNK], F32, tag="bank")
+            y = psum.tile([P, CHUNK], F32, tag="bank", name="y") if into is None else into
             nc.tensor.matmul_mx(
                 out=y[:],
                 lhsT=w_codes[:, feats].bitcast(FP8X4),
@@ -253,6 +256,8 @@ def tile_graphconvolutionbatch_kernel(tc, H, W, gamma, beta, out):
             load(chunk + LOAD_BUFS)
         for chunk in range(N_CHUNKS):
             ahead = chunk + AHEAD
+            if chunk > 0:
+                square(chunk - 1)
             keep(chunk, multiply(chunk, KEPT))
             ys = [multiply(chunk, fb) for fb in range(KEPT)]
             for fb in range(KEPT):
@@ -261,8 +266,6 @@ def tile_graphconvolutionbatch_kernel(tc, H, W, gamma, beta, out):
                 quantise(ahead, turn(ahead))
                 if ahead + LOAD_BUFS < N_CHUNKS:
                     load(ahead + LOAD_BUFS)
-            if chunk > 0:
-                square(chunk - 1)
             if chunk == AHEAD:
                 nc.vector.tensor_copy(out=gb_rows_f32[:], in_=gb_rows[:])
             if chunk == AHEAD + 1:
@@ -284,20 +287,14 @@ def tile_graphconvolutionbatch_kernel(tc, H, W, gamma, beta, out):
         for fb in range(KEPT):
             nc.vector.bn_aggr(out=mean_var[:, fb, :], in_=stats[:, fb, :, :].rearrange("p j s -> p (j s)"))
         nc.scalar.activation(out=std[:, 0:KEPT], in_=mean_var[:, 0:KEPT, 1], func=ACT.Sqrt, bias=eps[:, 0:1])
-        nc.vector.tensor_mul(
-            out=weighed[:, :, 1, :],
-            in0=gb[:, :, 0, :],
-            in1=mean_var[:, :, 0].unsqueeze(1).to_broadcast([P, 2, F_BLOCKS]),
-        )
+        nc.vector.tensor_mul(out=weighed[:, 1, :], in0=gb[:, 0, :], in1=mean_var[:, :, 0])
         rstd = const.tile([P, F_BLOCKS], F32)
         nc.vector.reciprocal(out=rstd[:], in_=std[:])
-        coeffs = const.tile([P, 2, 2, F_BLOCKS], F32)
+        coeffs = const.tile([P, 2, F_BLOCKS], F32)
         nc.vector.tensor_mul(
-            out=coeffs[:].rearrange("p i s f -> p (i s) f"),
-            in0=weighed[:].rearrange("p i s f -> p (i s) f"),
-            in1=rstd[:].unsqueeze(1).to_broadcast([P, 4, F_BLOCKS]),
+            out=coeffs[:], in0=weighed[:], in1=rstd[:].unsqueeze(1).to_broadcast([P, 2, F_BLOCKS])
         )
-        nc.vector.tensor_sub(out=coeffs[:, :, 1, :], in0=gb[:, :, 1, :], in1=coeffs[:, :, 1, :])
+        nc.vector.tensor_sub(out=coeffs[:, 1, :], in0=gb[:, 1, :], in1=coeffs[:, 1, :])
 
         row_sums = {}
         evens = {}
@@ -306,26 +303,19 @@ def tile_graphconvolutionbatch_kernel(tc, H, W, gamma, beta, out):
         results = {}
 
         def norm_relu(chunk, fb, y):
-            for first, count, on_edge in column_runs(chunk):
-                coeff = coeffs[:, 1 if on_edge else 0, :, :]
-                if fb < tensor_blocks(chunk):
-                    at = fb * CHUNK_COLS + first
-                    runs = padded[chunk % N_PADDED][:].rearrange("p (g s) -> p g s", s=PITCH)
-                    z_out = runs[:, at : at + count, RUN_AT:PITCH]
-                    y_in = y.rearrange("p (q n) -> p q n", n=P)[:, first : first + count, :]
-                else:
-                    by_parity = split[chunk % N_PADDED][:, 0 : 2 * ODD_AT].rearrange("p (t w) -> p t w", t=2)
-                    at = (fb - tensor_blocks(chunk)) * HALF + first * ROWS
-                    z_out = by_parity[:, :, at : at + count * ROWS].rearrange("p t (m b) -> p t m b", b=BATCH)
-                    pairs = slice(first * ROW_PAIRS, (first + count) * ROW_PAIRS)
-                    y_in = y.rearrange("p (m t b) -> p t m b", t=2, b=BATCH)[:, :, pairs, :]
-                nc.scalar.activation(
-                    out=z_out,
-                    in_=y_in,
-                    func=ACT.Relu,
-                    bias=coeff[:, 1, fb : fb + 1],
-                    scale=coeff[:, 0, fb : fb + 1],
-                )
+            if fb < tensor_blocks(chunk):
+                at = fb * CHUNK_COLS
+                runs = padded[chunk % N_PADDED][:].rearrange("p (g s) -> p g s", s=PITCH)
+                z_out = runs[:, at : at + CHUNK_COLS, RUN_AT:PITCH]
+                y_in = y.rearrange("p (q n) -> p q n", n=P)
+            else:
+                at = (fb - tensor_blocks(chunk)) * HALF
+                by_parity = split[chunk % N_PADDED][:, 0 : 2 * ODD_AT].rearrange("p (t w) -> p t w", t=2)
+                z_out = by_parity[:, :, at : at + HALF].rearrange("p t (m b) -> p t m b", b=BATCH)
+                y_in = y.rearrange("p (m t b) -> p t m b", t=2, b=BATCH)
+            nc.scalar.activation(
+                out=z_out, in_=y_in, func=ACT.Relu, bias=coeffs[:, 1, fb : fb + 1], scale=coeffs[:, 0, fb : fb + 1]
+            )
 
         def factors(chunk):
             edge = [(first, CHUNK_COLS, (D4 / D6) / (D6 / D9)) for first, count, on_edge in column_runs(chunk) if on_edge]
@@ -350,15 +340,19 @@ def tile_graphconvolutionbatch_kernel(tc, H, W, gamma, beta, out):
 
         both_rows = {}
 
-        def sum_over_rows(chunk):
+        def pair_rows(chunk):
             z = split[chunk % N_PADDED]
-            both = halves.tile([P, VECTOR_BLOCKS, HALF], F32, name="both_rows")
-            total = sums.tile([P, VECTOR_BLOCKS, CHUNK], F32, name="total")
+            both = halves.tile([P, vector_blocks(chunk), HALF], F32, name="both_rows")
             for i in range(vector_blocks(chunk)):
                 at = i * HALF
                 nc.vector.tensor_add(
                     out=both[:, i, :], in0=z[:, at : at + HALF], in1=z[:, at + ODD_AT : at + ODD_AT + HALF]
                 )
+            both_rows[chunk] = both
+
+        def sum_over_rows(chunk):
+            z, both = split[chunk % N_PADDED], both_rows[chunk]
+            total = sums.tile([P, vector_blocks(chunk), CHUNK], F32, name="total")
             for i in range(vector_blocks(chunk)):
                 at = i * HALF + BATCH
                 outer = (
@@ -372,7 +366,6 @@ def tile_graphconvolutionbatch_kernel(tc, H, W, gamma, beta, out):
                     in1=outer,
                 )
             row_sums[chunk] = total
-            both_rows[chunk] = both
 
         def mend_row_ends(chunk):
             ends = row_sums[chunk][:].rearrange("p i (q n) -> p (i q) n", n=P)
@@ -418,12 +411,15 @@ def tile_graphconvolutionbatch_kernel(tc, H, W, gamma, beta, out):
 
         def take_even(e):
             evens[e] = columns.tile([P, OUT_DIM], F32, name="even")
-            nc.scalar.activation(out=evens[e][:], in_=banks[2 * e][:], func=ACT.Copy, scale=row_factor[:, 0:1])
+            nc.scalar.activation(out=evens[e][:], in_=banks[2 * e][:], func=ACT.Copy, scale=edge_source[:, 0:1] if e == 0 else row_factor[:, 0:1])
 
         def add_pair(e):
             boths[e] = columns.tile([P, OUT_DIM], F32, name="both_columns")
             nc.vector.scalar_tensor_tensor(
-                out=boths[e][:], in0=banks[2 * e + 1][:], scalar=row_factor[:, 0:1], in1=evens[e][:],
+                out=boths[e][:],
+                in0=banks[2 * e + 1][:],
+                scalar=edge_source[:, 0:1] if 2 * e + 1 == COLS - 1 else row_factor[:, 0:1],
+                in1=evens[e][:],
                 op0=ALU.mult, op1=ALU.add,
             )
 
@@ -436,11 +432,17 @@ def tile_graphconvolutionbatch_kernel(tc, H, W, gamma, beta, out):
                     op0=ALU.mult, op1=ALU.add,
                 )
 
-        def finish_odd(e):
+        def finish_odd(e, on_vector):
             if e == COLS // 2 - 1:
                 nc.vector.tensor_scalar_mul(out=result_of(2 * e + 1), in0=boths[e][:], scalar1=column_factor[:, 0:1])
             else:
-                nc.gpsimd.tensor_add(out=result_of(2 * e + 1), in0=boths[e][:], in1=evens[e + 1][:])
+                if on_vector:
+                    nc.vector.scalar_tensor_tensor(
+                        out=result_of(2 * e + 1), in0=banks[2 * e + 2][:], scalar=row_factor[:, 0:1], in1=boths[e][:],
+                        op0=ALU.mult, op1=ALU.add,
+                    )
+                else:
+                    nc.gpsimd.tensor_add(out=result_of(2 * e + 1), in0=boths[e][:], in1=evens[e + 1][:])
             group, last = (2 * e + 1) // CHUNK_COLS, (2 * e + 1) % CHUNK_COLS + 1
             if group == N_CHUNKS - 1:
                 store(group, last - 2, last)
@@ -449,58 +451,53 @@ def tile_graphconvolutionbatch_kernel(tc, H, W, gamma, beta, out):
 
         products = {}
 
-        def multiply_again(chunk, some):
+        def multiply_again(chunk):
             if chunk < N_CHUNKS:
-                for fb in some:
+                for fb in PSUM_ORDER:
                     products[chunk, fb] = multiply(chunk, fb)[:]
                 products[chunk, KEPT] = y_kept[:, chunk * CHUNK : (chunk + 1) * CHUNK]
 
-        def sum_rows(chunk):
-            sum_over_rows(chunk)
-            mend_row_ends(chunk)
+        def norm(chunk, fb):
+            if chunk < N_CHUNKS:
+                norm_relu(chunk, fb, products[chunk, fb])
 
-        multiply_again(0, PSUM_ORDER)
+        multiply_again(0)
         for step in range(N_CHUNKS + LAG):
             new, last = step, step - 1
-            old = {1: 0, 2: -1}.get(step, step - LAG)
-            on_vector = new < N_CHUNKS and vector_blocks(new) > 0
-            if old >= 0:
-                e = old * CHUNK_COLS // 2
+            old = 0 if step == 1 else step - LAG if step > LAG else None
+            e = None if old is None else old * CHUNK_COLS // 2
+            norm(new, 3)
+            norm(new, 2)
+            if new < N_CHUNKS and vector_blocks(new) > 0:
+                scale_split(new)
+                pair_rows(new)
+                sum_over_rows(new)
+                mend_row_ends(new)
+            if e is not None:
                 turn_back(2 * e)
-                turn_back(2 * e + 1)
-            if new < N_CHUNKS:
-                norm_relu(new, 2, products[new, 2])
+                take_even(e)
             if 0 < last < N_CHUNKS:
                 scale_padded(last)
-            if new < N_CHUNKS:
-                norm_relu(new, 3, products[new, 3])
-            if step == 1:
-                scale_split(new)
-                sum_rows(new)
-            if old >= 0:
-                take_even(e)
-                add_pair(e)
+            norm(new, 0)
+            if e is not None:
                 if e > 0:
-                    finish_odd(e - 1)
-            multiply_again(new + 1, PSUM_ORDER[:2])
-            if old >= 0:
+                    finish_odd(e - 1, on_vector=False)
                 turn_back(2 * e + 2)
-                turn_back(2 * e + 3)
-            if on_vector and step > 1:
-                scale_split(new)
-            if new < N_CHUNKS:
-                norm_relu(new, 0, products[new, 0])
-            if old >= 0:
                 take_even(e + 1)
+            norm(new, 1)
+            if new == 0:
+                scale_padded(0)
+            if e is not None:
+                turn_back(2 * e + 1)
+                add_pair(e)
+                turn_back(2 * e + 3)
                 add_pair(e + 1)
                 finish_even(e)
-                finish_odd(e)
+                finish_odd(e, on_vector=True)
                 finish_even(e + 1)
-            if on_vector and step > 1:
-                sum_rows(new)
-            if new < N_CHUNKS:
-                norm_relu(new, 1, products[new, 1])
-                if new == 0:
-                    scale_padded(0)
-            multiply_again(new + 1, PSUM_ORDER[2:])
-        finish_odd(COLS // 2 - 1)
+            multiply_again(new + 1)
+            if new == 0:
+                idle = psum.tile([P, CHUNK], F32, tag="bank", name="idle")
+                for i in range(IDLE_PASSES):
+                    multiply(0, i % KEPT, into=idle)
+        finish_odd(COLS // 2 - 1, on_vector=True)

@@ -30,10 +30,10 @@ RUN_AT = 4
 HALF = CHUNK // 2
 N_PADDED = 4
 KEPT = F_BLOCKS - 1
-PSUM_ORDER = (2, 0, 1)
-IDLE_PASSES = 20
-VECTOR_BLOCKS = 2
-ODD_AT = VECTOR_BLOCKS * HALF + 8
+PSUM_ORDER = (2, 1, 0)
+IDLE_PASSES = 16
+ROW_BLOCKS = 2
+ODD_AT = ROW_BLOCKS * HALF + 8
 SPLIT = 2 * ODD_AT + HALF + 8
 LOAD_BUFS = 6
 AHEAD = 2
@@ -46,12 +46,12 @@ D4 = (4.0 + EPS_DEG) ** -0.5
 FLOPS = 2 * NODES * IN_DIM * OUT_DIM
 
 
-def vector_blocks(chunk):
-    return 0 if chunk in (0, N_CHUNKS - 1) else VECTOR_BLOCKS - (chunk % 3 == 2)
+def row_blocks(chunk):
+    return 0 if chunk in (0, N_CHUNKS - 1) else ROW_BLOCKS - chunk % 2
 
 
 def tensor_blocks(chunk):
-    return F_BLOCKS - vector_blocks(chunk)
+    return F_BLOCKS - row_blocks(chunk)
 
 
 def column_runs(chunk):
@@ -173,7 +173,7 @@ def tile_graphconvolutionbatch_kernel(tc, H, W, gamma, beta, out):
             nc.gpsimd.memset(pad_tile[:].rearrange("p (g s) -> p g s", s=PITCH)[:, :, 0:RUN_AT], 0.0)
             padded.append(pad_tile)
             split_tile = const.tile([P, SPLIT], F32, name="split%d" % i)
-            for block in range(VECTOR_BLOCKS):
+            for block in range(ROW_BLOCKS):
                 nc.gpsimd.memset(split_tile[:, (block + 1) * HALF : (block + 1) * HALF + BATCH], 0.0)
             nc.gpsimd.memset(split_tile[:, ODD_AT - BATCH : ODD_AT], 0.0)
             split.append(split_tile)
@@ -304,56 +304,53 @@ def tile_graphconvolutionbatch_kernel(tc, H, W, gamma, beta, out):
 
         def norm_relu(chunk, fb, y):
             if fb < tensor_blocks(chunk):
-                at = fb * CHUNK_COLS
+                n_blocks = tensor_blocks(chunk)
                 runs = padded[chunk % N_PADDED][:].rearrange("p (g s) -> p g s", s=PITCH)
-                z_out = runs[:, at : at + CHUNK_COLS, RUN_AT:PITCH]
+                z_out = runs[:, fb : n_blocks * CHUNK_COLS : n_blocks, RUN_AT:PITCH]
                 y_in = y.rearrange("p (q n) -> p q n", n=P)
             else:
                 at = (fb - tensor_blocks(chunk)) * HALF
                 by_parity = split[chunk % N_PADDED][:, 0 : 2 * ODD_AT].rearrange("p (t w) -> p t w", t=2)
                 z_out = by_parity[:, :, at : at + HALF].rearrange("p t (m b) -> p t m b", b=BATCH)
                 y_in = y.rearrange("p (m t b) -> p t m b", t=2, b=BATCH)
-            nc.scalar.activation(
-                out=z_out, in_=y_in, func=ACT.Relu, bias=coeffs[:, 1, fb : fb + 1], scale=coeffs[:, 0, fb : fb + 1]
-            )
-
-        def factors(chunk):
-            edge = [(first, CHUNK_COLS, (D4 / D6) / (D6 / D9)) for first, count, on_edge in column_runs(chunk) if on_edge]
-            return [(0, 1, D6 / D9)] + edge
+            gain, shift = coeffs[:, 0, fb : fb + 1], coeffs[:, 1, fb : fb + 1]
+            if chunk == 0 and fb == KEPT:
+                nc.vector.tensor_scalar(out=z_out, in0=y_in, scalar1=gain, scalar2=shift, op0=ALU.mult, op1=ALU.add)
+                nc.vector.tensor_scalar_max(out=z_out, in0=z_out, scalar1=0.0)
+            else:
+                nc.scalar.activation(out=z_out, in_=y_in, func=ACT.Relu, bias=shift, scale=gain)
 
         def scale_split(chunk):
-            n_runs = vector_blocks(chunk) * CHUNK_COLS
+            n_runs = row_blocks(chunk) * CHUNK_COLS
             apart = ODD_AT + ROWS - BATCH
             ends = split[chunk % N_PADDED][:, 0 : 2 * apart].rearrange("p (t w) -> p t w", t=2)
             ends = ends[:, :, 0 : n_runs * ROWS].rearrange("p t (g n) -> p t g n", n=ROWS)[:, :, :, 0:BATCH]
-            for first, step, factor in factors(chunk):
-                some = ends[:, :, first:n_runs:step, :]
-                nc.scalar.mul(out=some, in_=some, mul=factor)
+            nc.scalar.mul(out=ends, in_=ends, mul=D6 / D9)
 
         def scale_padded(chunk):
-            n_runs = tensor_blocks(chunk) * CHUNK_COLS
+            n_blocks = tensor_blocks(chunk)
             runs = padded[chunk % N_PADDED][:].rearrange("p (g s) -> p g s", s=PITCH)
-            ends = runs[:, 0:n_runs, RUN_AT:PITCH].rearrange("p g (r b) -> p g r b", b=BATCH)
-            for first, step, factor in factors(chunk):
-                some = ends[:, first:n_runs:step, 0 : ROWS : ROWS - 1, :]
-                nc.scalar.mul(out=some, in_=some, mul=factor)
+            for first, count, on_edge in column_runs(chunk):
+                some = runs[:, first * n_blocks : (first + count) * n_blocks, RUN_AT:PITCH]
+                ends = some.rearrange("p g (r b) -> p g r b", b=BATCH)[:, :, 0 : ROWS : ROWS - 1, :]
+                nc.scalar.mul(out=ends, in_=ends, mul=D4 / D6 if on_edge else D6 / D9)
 
         both_rows = {}
 
         def pair_rows(chunk):
             z = split[chunk % N_PADDED]
-            both = halves.tile([P, vector_blocks(chunk), HALF], F32, name="both_rows")
-            for i in range(vector_blocks(chunk)):
+            both = halves.tile([P, row_blocks(chunk), HALF], F32, name="both_rows")
+            for i in range(row_blocks(chunk)):
                 at = i * HALF
-                nc.vector.tensor_add(
+                nc.gpsimd.tensor_add(
                     out=both[:, i, :], in0=z[:, at : at + HALF], in1=z[:, at + ODD_AT : at + ODD_AT + HALF]
                 )
             both_rows[chunk] = both
 
         def sum_over_rows(chunk):
             z, both = split[chunk % N_PADDED], both_rows[chunk]
-            total = sums.tile([P, vector_blocks(chunk), CHUNK], F32, name="total")
-            for i in range(vector_blocks(chunk)):
+            total = sums.tile([P, row_blocks(chunk), CHUNK], F32, name="total")
+            for i in range(row_blocks(chunk)):
                 at = i * HALF + BATCH
                 outer = (
                     z[:, at : at + 2 * (ODD_AT - 2 * BATCH)]
@@ -379,10 +376,10 @@ def tile_graphconvolutionbatch_kernel(tc, H, W, gamma, beta, out):
             pad_tile = padded[chunk % N_PADDED]
             parts = []
             for fb in range(tensor_blocks(chunk)):
-                at = (fb * CHUNK_COLS + col) * PITCH + RUN_AT
+                at = (col * tensor_blocks(chunk) + fb) * PITCH + RUN_AT
                 for shift in (-BATCH, 0, BATCH):
                     parts.append((fb, pad_tile[:, at + shift : at + shift + P]))
-            for i in range(vector_blocks(chunk)):
+            for i in range(row_blocks(chunk)):
                 parts.append((tensor_blocks(chunk) + i, row_sums[chunk][:, i, col * P : (col + 1) * P]))
             bank = psum.tile([P, OUT_DIM], F32, tag="bank", name="bank")
             for i, (fb, source) in enumerate(parts):
@@ -431,6 +428,8 @@ def tile_graphconvolutionbatch_kernel(tc, H, W, gamma, beta, out):
                     out=result_of(2 * e), in0=banks[2 * e - 1][:], scalar=row_factor[:, 0:1], in1=boths[e][:],
                     op0=ALU.mult, op1=ALU.add,
                 )
+            if e == COLS // 2 - 1:
+                store(N_CHUNKS - 1, CHUNK_COLS - 2, CHUNK_COLS - 1)
 
         def finish_odd(e, on_vector):
             if e == COLS // 2 - 1:
@@ -444,10 +443,7 @@ def tile_graphconvolutionbatch_kernel(tc, H, W, gamma, beta, out):
                 else:
                     nc.gpsimd.tensor_add(out=result_of(2 * e + 1), in0=boths[e][:], in1=evens[e + 1][:])
             group, last = (2 * e + 1) // CHUNK_COLS, (2 * e + 1) % CHUNK_COLS + 1
-            if group == N_CHUNKS - 1:
-                store(group, last - 2, last)
-            elif last == CHUNK_COLS:
-                store(group, 0, CHUNK_COLS)
+            store(group, last - (1 if e == COLS // 2 - 1 else 2), last)
 
         products = {}
 
@@ -466,35 +462,36 @@ def tile_graphconvolutionbatch_kernel(tc, H, W, gamma, beta, out):
             new, last = step, step - 1
             old = 0 if step == 1 else step - LAG if step > LAG else None
             e = None if old is None else old * CHUNK_COLS // 2
+            has_rows = new < N_CHUNKS and row_blocks(new) > 0
             norm(new, 3)
+            if 0 < last < N_CHUNKS:
+                scale_padded(last)
             norm(new, 2)
-            if new < N_CHUNKS and vector_blocks(new) > 0:
+            if has_rows:
                 scale_split(new)
                 pair_rows(new)
-                sum_over_rows(new)
-                mend_row_ends(new)
             if e is not None:
                 turn_back(2 * e)
                 take_even(e)
-            if 0 < last < N_CHUNKS:
-                scale_padded(last)
-            norm(new, 0)
-            if e is not None:
-                if e > 0:
-                    finish_odd(e - 1, on_vector=False)
-                turn_back(2 * e + 2)
-                take_even(e + 1)
             norm(new, 1)
+            norm(new, 0)
             if new == 0:
                 scale_padded(0)
             if e is not None:
+                if e > 0:
+                    finish_odd(e - 1, on_vector=False)
                 turn_back(2 * e + 1)
                 add_pair(e)
+                finish_even(e)
+                turn_back(2 * e + 2)
+                take_even(e + 1)
                 turn_back(2 * e + 3)
                 add_pair(e + 1)
-                finish_even(e)
                 finish_odd(e, on_vector=True)
                 finish_even(e + 1)
+            if has_rows:
+                sum_over_rows(new)
+                mend_row_ends(new)
             multiply_again(new + 1)
             if new == 0:
                 idle = psum.tile([P, CHUNK], F32, tag="bank", name="idle")

from contextlib import ExitStack

import concourse.mybir as mybir
from concourse.masks import make_identity

F32 = mybir.dt.float32
BF16 = mybir.dt.bfloat16
U32 = mybir.dt.uint32
U8 = mybir.dt.uint8
FP8X4 = mybir.dt.float8_e4m3fn_x4
ACT = mybir.ActivationFunctionType
ALU = mybir.AluOpType
AXIS = mybir.AxisListType

P = 128
BATCH, ROWS, COLS = 2, 64, 64
IN_DIM, OUT_DIM = 512, 512
NODES = BATCH * ROWS * COLS
EPS_BN = 1e-5
EPS_DEG = 1e-5

PACK = 4
F_BLOCKS = OUT_DIM // P
CHUNK_COLS = 4
CHUNK = CHUNK_COLS * P
N_CHUNKS = COLS // CHUNK_COLS
ROW_PAIRS = ROWS // 2
PITCH = P + 4
RUN_AT = 4
HALF = CHUNK // 2
N_PADDED = 4
KEPT = F_BLOCKS - 1
PSUM_ORDER = (2, 1, 0)
IDLE_PASSES = 16
ROW_BLOCKS = 2
ODD_AT = ROW_BLOCKS * HALF + 8
SPLIT = 2 * ODD_AT + HALF + 8
LOAD_BUFS = 6
AHEAD = 2
LAG = 2

D9 = (9.0 + EPS_DEG) ** -0.5
D6 = (6.0 + EPS_DEG) ** -0.5
D4 = (4.0 + EPS_DEG) ** -0.5

FLOPS = 2 * NODES * IN_DIM * OUT_DIM


def row_blocks(chunk):
    return 0 if chunk in (0, N_CHUNKS - 1) else ROW_BLOCKS - chunk % 2


def tensor_blocks(chunk):
    return F_BLOCKS - row_blocks(chunk)


def column_runs(chunk):
    if chunk == 0:
        return [(0, 1, True), (1, CHUNK_COLS - 1, False)]
    if chunk == N_CHUNKS - 1:
        return [(0, CHUNK_COLS - 1, False), (CHUNK_COLS - 1, 1, True)]
    return [(0, CHUNK_COLS, False)]


def tile_graphconvolutionbatch_kernel(tc, H, W, gamma, beta, out):
    nc = tc.nc
    h_view = H.rearrange("b (r c) k -> (b r) c k", c=COLS)
    out_view = out.rearrange("b (r c) f -> b r c f", c=COLS)

    with ExitStack() as ctx:
        const = ctx.enter_context(tc.tile_pool(name="const", bufs=1))
        loads = ctx.enter_context(tc.tile_pool(name="loads", bufs=LOAD_BUFS))
        stage = ctx.enter_context(tc.tile_pool(name="stage", bufs=3))
        sums = ctx.enter_context(tc.tile_pool(name="sums", bufs=4))
        halves = ctx.enter_context(tc.tile_pool(name="halves", bufs=2))
        columns = ctx.enter_context(tc.tile_pool(name="columns", bufs=4))
        stores = ctx.enter_context(tc.tile_pool(name="stores", bufs=3))
        psum = ctx.enter_context(tc.psum_pool(name="psum", bufs=8))

        h_raw = {}

        def load(chunk):
            h_raw[chunk] = loads.tile([P, CHUNK_COLS, IN_DIM], BF16, name="h_raw")
            load_columns(chunk, 0, CHUNK_COLS)

        def load_columns(chunk, first, last):
            nc.sync.dma_start(
                out=h_raw[chunk][:, first:last, :],
                in_=h_view[:, chunk * CHUNK_COLS + first : chunk * CHUNK_COLS + last, :],
            )

        ctx.enter_context(tc.manual_schedule())

        h_raw[0] = loads.tile([P, CHUNK_COLS, IN_DIM], BF16, name="h_raw")
        load_columns(0, 0, CHUNK_COLS // 2)
        w_raw = const.tile([P, PACK, OUT_DIM], BF16)
        nc.sync.dma_start(out=w_raw[:], in_=W.rearrange("(p t) f -> p t f", t=PACK))
        load_columns(0, CHUNK_COLS // 2, CHUNK_COLS)
        for chunk in range(1, LOAD_BUFS):
            load(chunk)
        gb_rows = const.tile([P, P], BF16)
        nc.vector.memset(gb_rows[:], 0.0)
        nc.scalar.dma_start(out=gb_rows[0:F_BLOCKS, :], in_=gamma.rearrange("(j p) -> j p", p=P))
        nc.scalar.dma_start(
            out=gb_rows[F_BLOCKS : 2 * F_BLOCKS, :], in_=beta.rearrange("(j p) -> j p", p=P)
        )
        one = const.tile([P, 1], F32)
        nc.vector.memset(one[:], 1.0)
        root = const.tile([P, 1], F32)
        nc.scalar.sqrt(out=root[:], in_=one[:])
        eps = const.tile([P, 1], F32)
        nc.vector.tensor_scalar_mul(out=eps[:], in0=one[:], scalar1=EPS_BN)

        ident = const.tile([P, P], F32)
        make_identity(nc, ident[:])
        by_row = const.tile([P, P], F32)
        nc.vector.tensor_copy(
            out=by_row[:].rearrange("p (r b) -> p b r", b=BATCH),
            in_=ident[:].rearrange("p (b r) -> p b r", b=BATCH),
        )

        w_grouped = const.tile([P, OUT_DIM, PACK], BF16, align_bytes=64)
        w_codes = const.tile([P, OUT_DIM], U32, align_bytes=64)
        w_scales = const.tile([P, OUT_DIM], U8, align_bytes=64)
        gb_rows_f32 = const.tile([P, P], F32)
        gb = const.tile([P, 2, F_BLOCKS], F32)
        weighed = const.tile([P, 2, F_BLOCKS], F32)

        def quantise_weights():
            nc.vector.tensor_copy(out=w_grouped[:], in_=w_raw[:].rearrange("p t f -> p f t"))
            nc.vector.quantize_mx(
                out=w_codes[:].bitcast(FP8X4),
                scales=w_scales[:],
                in_=w_grouped[:].rearrange("p f t -> p (f t)"),
            )

        def turn_gamma_beta():
            bank = psum.tile([P, P], F32, tag="bank", name="gb_bank")
            nc.tensor.transpose(bank[:], gb_rows_f32[:], ident[:])
            nc.vector.tensor_scalar_mul(
                out=gb[:], in0=bank[:, 0 : 2 * F_BLOCKS].rearrange("p (s f) -> p s f", s=2), scalar1=D9 * D9
            )
            nc.vector.tensor_copy(out=weighed[:, 0, :], in_=gb[:, 0, :])

        on_row_edge = const.tile([P, 1], F32)
        nc.vector.tensor_reduce(
            out=on_row_edge[:],
            in_=ident[:].rearrange("p (r b) -> p r b", b=BATCH)[:, 0 : ROWS : ROWS - 1, :],
            axis=AXIS.XY,
            op=ALU.add,
        )
        row_factor = const.tile([P, 1], F32)
        nc.vector.tensor_scalar(
            out=row_factor[:], in0=on_row_edge[:], scalar1=D6 / D9 - 1.0, scalar2=1.0, op0=ALU.mult, op1=ALU.add
        )
        column_factor = const.tile([P, 1], F32)
        nc.vector.tensor_scalar(
            out=column_factor[:],
            in0=on_row_edge[:],
            scalar1=D4 / D6 - D6 / D9,
            scalar2=D6 / D9,
            op0=ALU.mult,
            op1=ALU.add,
        )

        edge_source = const.tile([P, 1], F32)
        nc.vector.tensor_scalar_mul(out=edge_source[:], in0=row_factor[:], scalar1=D6 / D9)

        padded = []
        split = []
        for i in range(N_PADDED):
            pad_tile = const.tile([P, (F_BLOCKS * CHUNK_COLS + 1) * PITCH], F32, name="padded%d" % i)
            nc.gpsimd.memset(pad_tile[:].rearrange("p (g s) -> p g s", s=PITCH)[:, :, 0:RUN_AT], 0.0)
            padded.append(pad_tile)
            split_tile = const.tile([P, SPLIT], F32, name="split%d" % i)
            for block in range(ROW_BLOCKS):
                nc.gpsimd.memset(split_tile[:, (block + 1) * HALF : (block + 1) * HALF + BATCH], 0.0)
            nc.gpsimd.memset(split_tile[:, ODD_AT - BATCH : ODD_AT], 0.0)
            split.append(split_tile)

        h_codes = const.tile([P, NODES], U32, align_bytes=64)
        h_scales = const.tile([P, NODES], U8, align_bytes=64)
        stats = const.tile([P, KEPT, N_CHUNKS, 6], F32)
        y_kept = const.tile([P, NODES], F32)
        kept_sums = const.tile([P, N_CHUNKS, 2], F32)
        kept_totals = const.tile([P, 2], F32)
        minus_first = const.tile([P, 1], F32)
        squares = const.tile([P, CHUNK], F32)

        def multiply(chunk, fb, into=None):
            nodes = slice(chunk * CHUNK, (chunk + 1) * CHUNK)
            feats = slice(fb * P, (fb + 1) * P)
            y = psum.tile([P, CHUNK], F32, tag="bank", name="y") if into is None else into
            nc.tensor.matmul_mx(
                out=y[:],
                lhsT=w_codes[:, feats].bitcast(FP8X4),
                lhsT_scale=w_scales[:, feats],
                rhs=h_codes[:, nodes].bitcast(FP8X4),
                rhs_scale=h_scales[:, nodes],
                start=True,
                stop=True,
            )
            return y

        def turn(chunk):
            grouped = stage.tile([P, CHUNK * PACK], BF16, align_bytes=64, name="grouped")
            grouped_words = grouped[:].bitcast(F32).rearrange("p (n u) -> p n u", u=2)
            for half in range(2):
                turned = psum.tile([P, 2, 2 * P], F32, tag="bank", name="turned")
                for i in range(2):
                    words = h_raw[chunk][:, 2 * half + i, :].bitcast(F32)
                    for u in range(2):
                        nc.tensor.transpose(
                            turned[:, u, i * P : (i + 1) * P], words[:, u : 2 * P : 2], by_row[:]
                        )
                nc.scalar.copy(
                    out=grouped_words[:, half * 2 * P : (half + 1) * 2 * P, :],
                    in_=turned[:].rearrange("p u n -> p n u"),
                )
            return grouped

        def quantise(chunk, grouped):
            nodes = slice(chunk * CHUNK, (chunk + 1) * CHUNK)
            nc.vector.quantize_mx(
                out=h_codes[:, nodes].bitcast(FP8X4), scales=h_scales[:, nodes], in_=grouped[:]
            )

        def keep(chunk, y):
            nodes = slice(chunk * CHUNK, (chunk + 1) * CHUNK)
            nc.scalar.activation(
                out=y_kept[:, nodes], in_=y[:], func=ACT.Identity, accum_out=kept_sums[:, chunk, 0:1]
            )
            if chunk == 0:
                nc.scalar.mul(out=minus_first[:], in_=kept_sums[:, 0, 0:1], mul=-1.0 / CHUNK)

        def square(chunk):
            nodes = slice(chunk * CHUNK, (chunk + 1) * CHUNK)
            nc.scalar.activation(
                out=squares[:],
                in_=y_kept[:, nodes],
                func=ACT.Square,
                bias=minus_first[:, 0:1],
                accum_out=kept_sums[:, chunk, 1:2],
            )
            if chunk == 0:
                nc.gpsimd.tensor_copy(out=kept_totals[:], in_=kept_sums[:, 0, :])
            else:
                nc.gpsimd.tensor_add(out=kept_totals[:], in0=kept_totals[:], in1=kept_sums[:, chunk, :])

        groups = {}
        for chunk in range(AHEAD):
            groups[chunk] = turn(chunk)
            if chunk == 0:
                quantise_weights()
            quantise(chunk, groups[chunk])
            load(chunk + LOAD_BUFS)
        for chunk in range(N_CHUNKS):
            ahead = chunk + AHEAD
            if chunk > 0:
                square(chunk - 1)
            keep(chunk, multiply(chunk, KEPT))
            ys = [multiply(chunk, fb) for fb in range(KEPT)]
            for fb in range(KEPT):
                nc.vector.bn_stats(out=stats[:, fb, chunk, :], in_=ys[fb][:])
            if ahead < N_CHUNKS:
                quantise(ahead, turn(ahead))
                if ahead + LOAD_BUFS < N_CHUNKS:
                    load(ahead + LOAD_BUFS)
            if chunk == AHEAD:
                nc.vector.tensor_copy(out=gb_rows_f32[:], in_=gb_rows[:])
            if chunk == AHEAD + 1:
                turn_gamma_beta()
        square(N_CHUNKS - 1)

        mean_var = const.tile([P, F_BLOCKS, 2], F32)
        std = const.tile([P, F_BLOCKS], F32)
        square_off = const.tile([P, 1], F32)
        eps_off = const.tile([P, 1], F32)
        nc.scalar.activation(
            out=square_off[:], in_=kept_totals[:, 0:1], func=ACT.Square, bias=minus_first[:, 0:1], scale=1.0 / NODES
        )
        nc.scalar.mul(out=mean_var[:, KEPT, 0:1], in_=kept_totals[:, 0:1], mul=1.0 / NODES)
        nc.scalar.activation(out=eps_off[:], in_=square_off[:], func=ACT.Identity, bias=eps[:, 0:1], scale=-1.0)
        nc.scalar.activation(
            out=std[:, KEPT:F_BLOCKS], in_=kept_totals[:, 1:2], func=ACT.Sqrt, bias=eps_off[:, 0:1], scale=1.0 / NODES
        )
        for fb in range(KEPT):
            nc.vector.bn_aggr(out=mean_var[:, fb, :], in_=stats[:, fb, :, :].rearrange("p j s -> p (j s)"))
        nc.scalar.activation(out=std[:, 0:KEPT], in_=mean_var[:, 0:KEPT, 1], func=ACT.Sqrt, bias=eps[:, 0:1])
        nc.vector.tensor_mul(out=weighed[:, 1, :], in0=gb[:, 0, :], in1=mean_var[:, :, 0])
        rstd = const.tile([P, F_BLOCKS], F32)
        nc.vector.reciprocal(out=rstd[:], in_=std[:])
        coeffs = const.tile([P, 2, F_BLOCKS], F32)
        nc.vector.tensor_mul(
            out=coeffs[:], in0=weighed[:], in1=rstd[:].unsqueeze(1).to_broadcast([P, 2, F_BLOCKS])
        )
        nc.vector.tensor_sub(out=coeffs[:, 1, :], in0=gb[:, 1, :], in1=coeffs[:, 1, :])

        row_sums = {}
        evens = {}
        boths = {}
        banks = {}
        results = {}

        def norm_relu(chunk, fb, y):
            if fb < tensor_blocks(chunk):
                n_blocks = tensor_blocks(chunk)
                runs = padded[chunk % N_PADDED][:].rearrange("p (g s) -> p g s", s=PITCH)
                z_out = runs[:, fb : n_blocks * CHUNK_COLS : n_blocks, RUN_AT:PITCH]
                y_in = y.rearrange("p (q n) -> p q n", n=P)
            else:
                at = (fb - tensor_blocks(chunk)) * HALF
                by_parity = split[chunk % N_PADDED][:, 0 : 2 * ODD_AT].rearrange("p (t w) -> p t w", t=2)
                z_out = by_parity[:, :, at : at + HALF].rearrange("p t (m b) -> p t m b", b=BATCH)
                y_in = y.rearrange("p (m t b) -> p t m b", t=2, b=BATCH)
            gain, shift = coeffs[:, 0, fb : fb + 1], coeffs[:, 1, fb : fb + 1]
            if chunk == 0 and fb == KEPT:
                nc.vector.tensor_scalar(out=z_out, in0=y_in, scalar1=gain, scalar2=shift, op0=ALU.mult, op1=ALU.add)
                nc.vector.tensor_scalar_max(out=z_out, in0=z_out, scalar1=0.0)
            else:
                nc.scalar.activation(out=z_out, in_=y_in, func=ACT.Relu, bias=shift, scale=gain)

        def scale_split(chunk):
            n_runs = row_blocks(chunk) * CHUNK_COLS
            apart = ODD_AT + ROWS - BATCH
            ends = split[chunk % N_PADDED][:, 0 : 2 * apart].rearrange("p (t w) -> p t w", t=2)
            ends = ends[:, :, 0 : n_runs * ROWS].rearrange("p t (g n) -> p t g n", n=ROWS)[:, :, :, 0:BATCH]
            nc.scalar.mul(out=ends, in_=ends, mul=D6 / D9)

        def scale_padded(chunk):
            n_blocks = tensor_blocks(chunk)
            runs = padded[chunk % N_PADDED][:].rearrange("p (g s) -> p g s", s=PITCH)
            for first, count, on_edge in column_runs(chunk):
                some = runs[:, first * n_blocks : (first + count) * n_blocks, RUN_AT:PITCH]
                ends = some.rearrange("p g (r b) -> p g r b", b=BATCH)[:, :, 0 : ROWS : ROWS - 1, :]
                nc.scalar.mul(out=ends, in_=ends, mul=D4 / D6 if on_edge else D6 / D9)

        both_rows = {}

        def pair_rows(chunk):
            z = split[chunk % N_PADDED]
            both = halves.tile([P, row_blocks(chunk), HALF], F32, name="both_rows")
            for i in range(row_blocks(chunk)):
                at = i * HALF
                nc.gpsimd.tensor_add(
                    out=both[:, i, :], in0=z[:, at : at + HALF], in1=z[:, at + ODD_AT : at + ODD_AT + HALF]
                )
            both_rows[chunk] = both

        def sum_over_rows(chunk):
            z, both = split[chunk % N_PADDED], both_rows[chunk]
            total = sums.tile([P, row_blocks(chunk), CHUNK], F32, name="total")
            for i in range(row_blocks(chunk)):
                at = i * HALF + BATCH
                outer = (
                    z[:, at : at + 2 * (ODD_AT - 2 * BATCH)]
                    .rearrange("p (t w) -> p t w", t=2)[:, ::-1, 0:HALF]
                    .rearrange("p t (m b) -> p m t b", b=BATCH)
                )
                nc.vector.tensor_add(
                    out=total[:, i, :].rearrange("p (m t b) -> p m t b", t=2, b=BATCH),
                    in0=both[:, i, :].rearrange("p (m b) -> p m b", b=BATCH).unsqueeze(2).to_broadcast([P, HALF // BATCH, 2, BATCH]),
                    in1=outer,
                )
            row_sums[chunk] = total

        def mend_row_ends(chunk):
            ends = row_sums[chunk][:].rearrange("p i (q n) -> p (i q) n", n=P)
            ends = ends.rearrange("p g (r b) -> p g r b", b=BATCH)[:, :, 0 : ROWS : ROWS - 1, :]
            pairs = both_rows[chunk][:].rearrange("p i (q n) -> p (i q) n", q=CHUNK_COLS)
            pairs = pairs.rearrange("p g (k b) -> p g k b", b=BATCH)[:, :, 0 : ROW_PAIRS : ROW_PAIRS - 1, :]
            nc.gpsimd.tensor_copy(out=ends, in_=pairs)

        def turn_back(c):
            chunk, col = c // CHUNK_COLS, c % CHUNK_COLS
            pad_tile = padded[chunk % N_PADDED]
            parts = []
            for fb in range(tensor_blocks(chunk)):
                at = (col * tensor_blocks(chunk) + fb) * PITCH + RUN_AT
                for shift in (-BATCH, 0, BATCH):
                    parts.append((fb, pad_tile[:, at + shift : at + shift + P]))
            for i in range(row_blocks(chunk)):
                parts.append((tensor_blocks(chunk) + i, row_sums[chunk][:, i, col * P : (col + 1) * P]))
            bank = psum.tile([P, OUT_DIM], F32, tag="bank", name="bank")
            for i, (fb, source) in enumerate(parts):
                nc.tensor.matmul(
                    out=bank[:, fb * P : (fb + 1) * P],
                    lhsT=source,
                    rhs=ident[:],
                    is_transpose=True,
                    start=(i == 0),
                    stop=(i == len(parts) - 1),
                )
            banks[c] = bank

        def result_of(c):
            group = c // CHUNK_COLS
            if group not in results:
                results[group] = stores.tile([P, CHUNK_COLS, OUT_DIM], F32, name="result")
            return results[group][:, c % CHUNK_COLS, :]

        def store(group, first, last):
            for b in range(BATCH):
                nc.sync.dma_start(
                    out=out_view[b, :, group * CHUNK_COLS + first : group * CHUNK_COLS + last, :],
                    in_=results[group][b : P : BATCH, first:last, :],
                )

        def take_even(e):
            evens[e] = columns.tile([P, OUT_DIM], F32, name="even")
            nc.scalar.activation(out=evens[e][:], in_=banks[2 * e][:], func=ACT.Copy, scale=edge_source[:, 0:1] if e == 0 else row_factor[:, 0:1])

        def add_pair(e):
            boths[e] = columns.tile([P, OUT_DIM], F32, name="both_columns")
            nc.vector.scalar_tensor_tensor(
                out=boths[e][:],
                in0=banks[2 * e + 1][:],
                scalar=edge_source[:, 0:1] if 2 * e + 1 == COLS - 1 else row_factor[:, 0:1],
                in1=evens[e][:],
                op0=ALU.mult, op1=ALU.add,
            )

        def finish_even(e):
            if e == 0:
                nc.vector.tensor_scalar_mul(out=result_of(0), in0=boths[0][:], scalar1=column_factor[:, 0:1])
            else:
                nc.vector.scalar_tensor_tensor(
                    out=result_of(2 * e), in0=banks[2 * e - 1][:], scalar=row_factor[:, 0:1], in1=boths[e][:],
                    op0=ALU.mult, op1=ALU.add,
                )
            if e == COLS // 2 - 1:
                store(N_CHUNKS - 1, CHUNK_COLS - 2, CHUNK_COLS - 1)

        def finish_odd(e, on_vector):
            if e == COLS // 2 - 1:
                nc.vector.tensor_scalar_mul(out=result_of(2 * e + 1), in0=boths[e][:], scalar1=column_factor[:, 0:1])
            else:
                if on_vector:
                    nc.vector.scalar_tensor_tensor(
                        out=result_of(2 * e + 1), in0=banks[2 * e + 2][:], scalar=row_factor[:, 0:1], in1=boths[e][:],
                        op0=ALU.mult, op1=ALU.add,
                    )
                else:
                    nc.gpsimd.tensor_add(out=result_of(2 * e + 1), in0=boths[e][:], in1=evens[e + 1][:])
            group, last = (2 * e + 1) // CHUNK_COLS, (2 * e + 1) % CHUNK_COLS + 1
            store(group, last - (1 if e == COLS // 2 - 1 else 2), last)

        products = {}

        def multiply_again(chunk):
            if chunk < N_CHUNKS:
                for fb in PSUM_ORDER:
                    products[chunk, fb] = multiply(chunk, fb)[:]
                products[chunk, KEPT] = y_kept[:, chunk * CHUNK : (chunk + 1) * CHUNK]

        def norm(chunk, fb):
            if chunk < N_CHUNKS:
                norm_relu(chunk, fb, products[chunk, fb])

        multiply_again(0)
        for step in range(N_CHUNKS + LAG):
            new, last = step, step - 1
            old = 0 if step == 1 else step - LAG if step > LAG else None
            e = None if old is None else old * CHUNK_COLS // 2
            has_rows = new < N_CHUNKS and row_blocks(new) > 0
            norm(new, 3)
            if 0 < last < N_CHUNKS:
                scale_padded(last)
            norm(new, 2)
            if has_rows:
                scale_split(new)
                pair_rows(new)
            if e is not None:
                turn_back(2 * e)
                take_even(e)
            norm(new, 1)
            norm(new, 0)
            if new == 0:
                scale_padded(0)
            if e is not None:
                if e > 0:
                    finish_odd(e - 1, on_vector=False)
                turn_back(2 * e + 1)
                add_pair(e)
                finish_even(e)
                turn_back(2 * e + 2)
                take_even(e + 1)
                turn_back(2 * e + 3)
                add_pair(e + 1)
                finish_odd(e, on_vector=True)
                finish_even(e + 1)
            if has_rows:
                sum_over_rows(new)
                mend_row_ends(new)
            multiply_again(new + 1)
            if new == 0:
                idle = psum.tile([P, CHUNK], F32, tag="bank", name="idle")
                for i in range(IDLE_PASSES):
                    multiply(0, i % KEPT, into=idle)
        finish_odd(COLS // 2 - 1, on_vector=True)
